import numpy as np
import ml_dtypes


def mxq(x, axis, fmt="e4m3"):
    dtype, down = {"e4m3": (ml_dtypes.float8_e4m3fn, 7), "e5m2": (ml_dtypes.float8_e5m2, 14)}[fmt]
    v = np.moveaxis(np.asarray(x, np.float32).astype(ml_dtypes.bfloat16).astype(np.float64), axis, -1)
    blocks = v.reshape(v.shape[:-1] + (-1, 32))
    amax = np.abs(blocks).max(-1, keepdims=True)
    byte = np.maximum(np.where(amax > 0, np.frexp(amax)[1] - 1 + 127, 0) - down, 1)
    scale = np.exp2(byte - 127.0)
    codes = (blocks / scale).astype(np.float32).astype(dtype).astype(np.float64)
    return np.moveaxis((codes * scale).reshape(v.shape), -1, axis)


WIDE = False


def mx_kscale(k):
    if not WIDE:
        return np.ones(k)
    levels = np.array([30, -30])
    if k % 512:
        return np.exp2(np.random.permutation(np.resize(levels, k // 32))).repeat(32)
    a = np.empty((k // 512, 16))
    for p in range(k // 512):
        a[p, :8] = np.random.permutation(np.resize(levels, 8))
        for g in range(8):
            far = levels[np.abs(levels - a[p, g]) >= 10]
            a[p, g + 8] = far[np.random.randint(len(far))]
    return np.exp2(a.ravel()).repeat(32)


BF16 = ml_dtypes.bfloat16


def bf(x):
    return np.asarray(x, np.float32).astype(BF16)


def f64(x):
    return np.asarray(x).astype(np.float64)


E2M1 = np.array([0.0, 0.5, 1.0, 1.5, 2.0, 3.0, 4.0, 6.0, -0.0, -0.5, -1.0, -1.5, -2.0, -3.0, -4.0, -6.0])


def pack_weight(w, fmt):
    k, n = w.shape
    w = f64(bf(w)).reshape(k // 32, 32, n)
    amax = np.abs(w).max(1)
    if fmt == "e4m3":
        byte = np.frexp(amax)[1] - 1 + 127 - 7
    else:
        mant, ex = np.frexp(amax / 6.0)
        byte = np.where(mant > 0.5, ex, ex - 1) + 127
    byte = np.clip(np.where(amax > 0, byte, 1), 1, 254)
    scaled = (w * np.exp2(127.0 - byte)[:, None, :]).reshape(k, n).astype(np.float32)
    by_word = np.ascontiguousarray(scaled.reshape(k // 512, 128, 4, n).transpose(0, 1, 3, 2))
    if fmt == "e4m3":
        words = by_word.astype(ml_dtypes.float8_e4m3fn).view(np.uint8)
    else:
        c = by_word.astype(ml_dtypes.float4_e2m1fn).view(np.uint8) & 0xF
        words = c[..., 0::2] | (c[..., 1::2] << 4)
    return np.ascontiguousarray(words), np.ascontiguousarray(byte.astype(np.uint8).reshape(k // 512, 16, n))


def unpack_weight(words, scales, fmt):
    g, p, n, _ = words.shape
    if fmt == "e4m3":
        vals = np.ascontiguousarray(words).view(ml_dtypes.float8_e4m3fn).astype(np.float64)
    else:
        nib = np.empty((g, p, n, 4), np.uint8)
        nib[..., 0::2] = words & 0xF
        nib[..., 1::2] = words >> 4
        vals = E2M1[nib]
    vals = vals * np.repeat(np.exp2(scales.astype(np.float64) - 127.0), 8, axis=1)[..., None]
    return vals.transpose(0, 1, 3, 2).reshape(g * 512, n)

def pack4(w):
    words, scales = pack_weight(w, "e2m1")
    return words.reshape(words.shape[0], 128, -1), scales


def unpack4(words, scales):
    return unpack_weight(words.reshape(words.shape[0], 128, -1, 2), scales, "e2m1")


B, L, D, H, HD, MINI, NCH, TEXT, OFF = 4, 512, 1024, 16, 64, 64, 4, 64, 128


def rope_table():
    inv_freq = 1.0 / (10000.0 ** (np.arange(0, HD, 2) / HD))
    ang = np.outer(np.arange(L), inv_freq)
    return np.stack([np.cos(ang), np.sin(ang)], axis=-1)


def l2norm(x):
    return x / np.maximum(np.sqrt((x * x).sum(-1, keepdims=True)), 1e-12)


def rope(x, cos, sin):
    c = cos[None, :, None, :]
    s = sin[None, :, None, :]
    xr, xi = x[..., 0::2], x[..., 1::2]
    return np.stack([xr * c - xi * s, xr * s + xi * c], axis=-1).reshape(x.shape)


def setup_inputs():
    s = mx_kscale(D)
    hidden_states = bf(np.random.standard_normal((B, L, D)) * s)
    freqs_cis = bf(rope_table())
    wk_w_words, wk_w_scales = pack4(np.random.standard_normal((D, D)) / np.sqrt(D) / s[:, None])
    wk_b = bf(np.random.standard_normal(D) * 0.1)
    wv_w_words, wv_w_scales = pack4(np.random.standard_normal((D, D)) * 0.5 / np.sqrt(D) / s[:, None])
    wv_b = bf(np.random.standard_normal(D) * 0.1)
    ttt_norm_weight = bf(1.0 + 0.1 * np.random.standard_normal((H, HD)))
    ttt_norm_bias = bf(0.1 * np.random.standard_normal((H, HD)))
    return {"hidden_states": hidden_states,
            "freqs_cis": freqs_cis,
            "wk_w_words": wk_w_words,
            "wk_w_scales": wk_w_scales,
            "wk_b": wk_b,
            "wv_w_words": wv_w_words,
            "wv_w_scales": wv_w_scales,
            "wv_b": wv_b,
            "ttt_norm_weight": ttt_norm_weight,
            "ttt_norm_bias": ttt_norm_bias}


def reference(hidden_states, freqs_cis, wk_w_words, wk_w_scales, wk_b, wv_w_words, wv_w_scales, wv_b, ttt_norm_weight, ttt_norm_bias):
    hq = mxq(f64(hidden_states), 2, "e5m2")
    xk = ((hq @ unpack4(wk_w_words, wk_w_scales)) + f64(wk_b)).reshape(B, L, H, HD)
    xv = ((hq @ unpack4(wv_w_words, wv_w_scales)) + f64(wv_b)).reshape(B, L, H, HD)
    fc = f64(freqs_cis)
    xk = rope(l2norm(xk), fc[..., 0], fc[..., 1])
    diff = xv - xk
    mean = diff.mean(axis=-1, keepdims=True)
    std = diff.std(axis=-1, keepdims=True, ddof=1)
    norm = (diff - mean) / (std + 1e-8)
    xv = f64(ttt_norm_weight)[None, None] * norm + f64(ttt_norm_bias)[None, None] + xk
    return xk, xv

@@ -1,0 +1,392 @@
+from contextlib import ExitStack
+
+import concourse.mybir as mybir
+from concourse.masks import make_identity
+
+B, L, D, H, HD = 4, 512, 1024, 16, 64
+FLOPS = 2 * 2 * B * L * D * D
+
+F32 = mybir.dt.float32
+BF16 = mybir.dt.bfloat16
+I32 = mybir.dt.int32
+U32 = mybir.dt.uint32
+U8 = mybir.dt.uint8
+E5M2 = mybir.dt.float8_e5m2_x4
+E2M1 = mybir.dt.float4_e2m1fn_x4
+ALU = mybir.AluOpType
+ACT = mybir.ActivationFunctionType
+
+P = 128
+PASSES = D // 512
+TILES = L // P
+CHUNKS = D // P
+UNITS = B * CHUNKS
+HALF = 4
+LAST = 2
+
+
+def tile_tttwrapper_pa_kernel(tc, hidden_states, freqs_cis, wk_w_words, wk_w_scales, wk_b,
+                                          wv_w_words, wv_w_scales, wv_b, ttt_norm_weight, ttt_norm_bias,
+                                          out_0, out_1):
+    nc = tc.nc
+    xk_hbm = out_0.rearrange("b (i p) h d -> b p i (h d)", p=P)
+    xv_hbm = out_1.rearrange("b (i p) h d -> b p i (h d)", p=P)
+
+    with ExitStack() as ctx:
+        keep = ctx.enter_context(tc.tile_pool(name="keep", bufs=1))
+        work = ctx.enter_context(tc.tile_pool(name="work", bufs=3))
+        psum = ctx.enter_context(tc.psum_pool(name="psum", bufs=1))
+        ctx.enter_context(tc.manual_schedule())
+
+        planes = {}
+        for kv in ("k", "v"):
+            planes[kv] = keep.tile([P, PASSES, D], U8, name="plane_" + kv, align_bytes=64)
+            nc.vector.memset(planes[kv][:].rearrange("p g n -> p (g n)").bitcast(I32), 0)
+        rows = keep.tile([P, P], BF16, name="rows")
+        nc.vector.memset(rows[:], 0.0)
+
+        freqs = keep.tile([P, TILES, HD], BF16, name="freqs")
+        nc.scalar.dma_start(out=freqs[:], in_=freqs_cis.rearrange("(i p) j e -> p i (j e)", p=P))
+        nc.scalar.dma_start(out=rows[0:8, :], in_=wk_b.rearrange("(c m) -> c m", m=P))
+        nc.scalar.dma_start(out=rows[8:16, :], in_=wv_b.rearrange("(c m) -> c m", m=P))
+        nc.scalar.dma_start(out=rows[16:24, :], in_=ttt_norm_bias.rearrange("(c h) d -> c (h d)", h=2))
+        nc.scalar.dma_start(out=rows[24:32, :], in_=ttt_norm_weight.rearrange("(c h) d -> c (h d)", h=2))
+
+        x = {}
+
+        def load_x(b):
+            for i in range(TILES):
+                x[b, i] = keep.tile([P, D], BF16, name="x_%d_%d" % (b, i))
+                nc.sync.dma_start(out=x[b, i][:], in_=hidden_states[b, P * i : P * (i + 1), :])
+
+        words = {}
+
+        def load_words(kv, src, half):
+            words[kv, half] = keep.tile([P, PASSES, D], U8, name="words_%s_%d" % (kv, half), align_bytes=64)
+            nc.sync.dma_start(out=words[kv, half][:].bitcast(I32),
+                              in_=src[:, :, D * half : D * (half + 1)].rearrange("g p n -> p g n").bitcast(I32))
+
+        def load_scales(kv, src):
+            for q in range(4):
+                nc.sync.dma_start(out=planes[kv][32 * q : 32 * q + 4, :, :].bitcast(I32),
+                                  in_=src[:, 4 * q : 4 * q + 4, :].rearrange("g r n -> r g n").bitcast(I32))
+
+        load_x(0)
+        load_words("k", wk_w_words, 0)
+        load_scales("k", wk_w_scales)
+        load_scales("v", wv_w_scales)
+        load_words("v", wv_w_words, 0)
+        load_x(1)
+        load_words("k", wk_w_words, 1)
+        load_words("v", wv_w_words, 1)
+        load_x(2)
+        load_x(3)
+
+        ident = keep.tile([P, P], F32, name="ident")
+        make_identity(nc, ident[:])
+        ident_bf = keep.tile([P, P], BF16, name="ident_bf")
+        make_identity(nc, ident_bf[:])
+        swap = keep.tile([P, P], F32, name="swap")
+        for e in range(2):
+            nc.vector.tensor_copy(out=swap[:, e::2], in_=ident[:, 1 - e :: 2])
+        head_sum = keep.tile([P, 2], F32, name="head_sum")
+        nc.vector.memset(head_sum[:], 0.0)
+        nc.vector.memset(head_sum[0:HD, 0:1], 1.0)
+        nc.vector.memset(head_sum[HD:P, 1:2], 1.0)
+        sign = keep.tile([P, 2], F32, name="sign")
+        nc.vector.memset(sign[:, 0:1], 1.0)
+        nc.vector.memset(sign[:, 1:2], -1.0)
+
+        spread = keep.tile([P, 2, TILES, P], BF16, name="spread")
+        pairs = freqs[:].rearrange("p i (j e) -> p i j e", e=2)
+        for h in range(2):
+            cols = slice(HD * h, HD * (h + 1))
+            nc.vector.tensor_copy(out=spread[:, 0, :, cols].rearrange("p i (j e) -> p i j e", e=2),
+                                  in_=pairs[:, :, :, 0:1].to_broadcast([P, TILES, HD // 2, 2]))
+            nc.vector.tensor_tensor(out=spread[:, 1, :, cols].rearrange("p i (j e) -> p i j e", e=2),
+                                    in0=pairs[:, :, :, 1:2].to_broadcast([P, TILES, HD // 2, 2]),
+                                    in1=sign[:].unsqueeze(1).unsqueeze(1).to_broadcast([P, TILES, HD // 2, 2]),
+                                    op=ALU.mult)
+
+        grouped, codes, scales = {}, {}, {}
+
+        def open_batch(b):
+            grouped[b] = work.tile([P, PASSES, 4 * L], BF16, name="grouped", bufs=2, align_bytes=64)
+            codes[b] = work.tile([P, PASSES, L], U32, name="codes", bufs=2, align_bytes=64)
+            scales[b] = work.tile([P, PASSES, L], U8, name="scales", bufs=2, align_bytes=64)
+
+        def turn(bank, b, i, g):
+            w = x[b, i][:].bitcast(F32)
+            for u in range(2):
+                nc.tensor.transpose(bank[:, u, :], w[:, 256 * g + u : 256 * (g + 1) : 2], ident[:])
+
+        def grouped_words(b, i, g):
+            return grouped[b][:, g, 4 * P * i : 4 * P * (i + 1)].bitcast(F32).rearrange("p (r u) -> p r u", u=2)
+
+        def quantise(b, g):
+            nc.vector.quantize_mx(out=codes[b][:, g, :].bitcast(E5M2), scales=scales[b][:, g, :], in_=grouped[b][:, g, :])
+
+        open_batch(0)
+        for i in range(TILES):
+            bank = psum.tile([P, PASSES, 2, P], F32, name="first_x", tag="u" if i < 2 else "k", bufs=2)
+            for g in range(PASSES):
+                turn(bank[:, g], 0, i, g)
+            for g in range(PASSES):
+                if i % 2 == 0:
+                    nc.scalar.copy(out=grouped_words(0, i, g), in_=bank[:, g].rearrange("p u r -> p r u"))
+                else:
+                    nc.vector.tensor_copy(out=grouped_words(0, i, g), in_=bank[:, g].rearrange("p u r -> p r u"))
+            if i == 1:
+                rows_t = psum.tile([P, P], BF16, name="rows_t", tag="ss")
+                nc.tensor.transpose(rows_t[:], rows[:], ident_bf[:])
+                table_t = psum.tile([P, 2, L], BF16, name="table_t", tag="vt")
+                for cs in range(2):
+                    for t in range(TILES):
+                        nc.tensor.transpose(table_t[:, cs, P * t : P * (t + 1)], spread[:, cs, t, :], ident_bf[:])
+        table = keep.tile([P, 2, L], BF16, name="table")
+        nc.scalar.copy(out=table[:], in_=table_t[:])
+        columns = keep.tile([P, 3 * CHUNKS], F32, name="columns")
+        nc.scalar.copy(out=columns[:], in_=rows_t[:, 0 : 3 * CHUNKS])
+        for g in range(PASSES):
+            quantise(0, g)
+        bias_v = keep.tile([P, CHUNKS], F32, name="bias_v")
+        nc.vector.tensor_tensor(out=bias_v[:], in0=columns[:, CHUNKS : 2 * CHUNKS], in1=columns[:, 2 * CHUNKS :], op=ALU.add)
+
+        def spread_rows(first_row, name, tags):
+            wide = keep.tile([P, D], F32, name=name)
+            for half in range(2):
+                bank = psum.tile([P, HALF, P], F32, name="spread_" + name, tag=tags[half])
+                for c in range(HALF):
+                    r = first_row + HALF * half + c
+                    nc.tensor.matmul(bank[:, c, :], lhsT=ident_bf[:, r : r + 1].to_broadcast([P, P]), rhs=rows[:],
+                                     start=True, stop=True)
+                nc.scalar.copy(out=wide[:, HALF * P * half : HALF * P * (half + 1)], in_=bank[:].rearrange("p c m -> p (c m)"))
+            return wide
+
+        beta = spread_rows(2 * CHUNKS, "beta", ("v", "xt"))
+        gamma = spread_rows(3 * CHUNKS, "gamma", ("ss", "vt"))
+
+        t = {}
+
+        def project(n):
+            b, c = divmod(n, CHUNKS)
+            for kv in ("k", "v"):
+                t[kv, n] = psum.tile([P, L], F32, name="proj_" + kv, tag=kv, bufs=2 if kv == "k" else 1)
+                for g in range(PASSES):
+                    nc.tensor.matmul_mx(
+                        out=t[kv, n][:],
+                        lhsT=words[kv, c // HALF][:, g, 2 * P * (c % HALF) : 2 * P * (c % HALF + 1)].bitcast(E2M1),
+                        lhsT_scale=planes[kv][:, g, P * c : P * (c + 1)],
+                        rhs=codes[b][:, g, :].bitcast(E5M2), rhs_scale=scales[b][:, g, :],
+                        start=(g == 0), stop=(g == PASSES - 1))
+
+        def rope_terms(n):
+            c = n % CHUNKS
+            t["terms", n] = work.tile([P, 2, L], F32, name="terms")
+            nc.vector.scalar_tensor_tensor(out=t["terms", n][:], in0=t["k", n][:].unsqueeze(1).to_broadcast([P, 2, L]),
+                                           scalar=columns[:, c : c + 1], in1=table[:], op0=ALU.add, op1=ALU.mult)
+
+        def squares(n):
+            c = n % CHUNKS
+            t["sq", n] = work.tile([P, L], F32, name="sq")
+            nc.scalar.activation(out=t["sq", n][:], in_=t["k", n][:], func=ACT.Square, bias=columns[:, c : c + 1])
+
+        def value(n):
+            c = n % CHUNKS
+            t["v0", n] = work.tile([P, L], F32, name="v0", bufs=4)
+            nc.scalar.activation(out=t["v0", n][:], in_=t["v", n][:], func=ACT.Identity, bias=bias_v[:, c : c + 1])
+
+        def sum_squares(n):
+            t["ss", n] = psum.tile([P, 2 * TILES], F32, name="ss", tag="ss")
+            for i in range(TILES):
+                nc.tensor.matmul(t["ss", n][:, 2 * i : 2 * i + 2], lhsT=t["sq", n][:, P * i : P * (i + 1)], rhs=head_sum[:],
+                                 start=True, stop=True)
+
+        def rotate(n):
+            t["u", n] = psum.tile([P, TILES, P], F32, name="u", tag="u", bufs=2)
+            for i in range(TILES):
+                cols = slice(P * i, P * (i + 1))
+                nc.tensor.matmul(t["u", n][:, i, :], lhsT=t["terms", n][:, 0, cols], rhs=ident[:], is_transpose=True,
+                                 start=True, stop=False)
+                nc.tensor.matmul(t["u", n][:, i, :], lhsT=t["terms", n][:, 1, cols], rhs=swap[:], is_transpose=True,
+                                 start=False, stop=True)
+
+        def turn_value(n):
+            t["vt", n] = psum.tile([P, TILES, P], F32, name="vt", tag="vt")
+            for i in range(TILES):
+                nc.tensor.transpose(t["vt", n][:, i, :], t["v0", n][:, P * i : P * (i + 1)], ident[:])
+
+        def norm_floor(n):
+            t["ssm", n] = work.tile([P, 2 * TILES], F32, name="ssm")
+            nc.vector.tensor_scalar(out=t["ssm", n][:], in0=t["ss", n][:], scalar1=1e-24, scalar2=None, op0=ALU.max)
+
+        def norm_root(n):
+            t["nrm", n] = work.tile([P, 2 * TILES], F32, name="nrm")
+            nc.scalar.activation(out=t["nrm", n][:], in_=t["ssm", n][:], func=ACT.Sqrt)
+
+        def norm_inverse(n):
+            t["r", n] = work.tile([P, 2 * TILES], F32, name="r")
+            nc.vector.reciprocal(out=t["r", n][:], in_=t["nrm", n][:])
+
+        def pair_tile(kind, n, bufs):
+            if n % 2 == 0:
+                t[kind, n // 2] = work.tile([P, TILES, 2 * P], F32, name=kind, bufs=bufs)
+            return t[kind, n // 2][:, :, P * (n % 2) : P * (n % 2 + 1)]
+
+        def key_plus_bias(n):
+            c = n % CHUNKS
+            dst = pair_tile("xkb", n, 4)
+            for i in range(TILES):
+                for h in range(2):
+                    cols = slice(HD * h, HD * (h + 1))
+                    nc.vector.scalar_tensor_tensor(out=dst[:, i, cols], in0=t["u", n][:, i, cols],
+                                                   scalar=t["r", n][:, 2 * i + h : 2 * i + h + 1],
+                                                   in1=beta[:, P * c + HD * h : P * c + HD * (h + 1)],
+                                                   op0=ALU.mult, op1=ALU.add)
+
+        def key(n):
+            dst = pair_tile("xk", n, 3)
+            for i in range(TILES):
+                for h in range(2):
+                    cols = slice(HD * h, HD * (h + 1))
+                    nc.scalar.activation(out=dst[:, i, cols], in_=t["u", n][:, i, cols], func=ACT.Copy,
+                                         scale=t["r", n][:, 2 * i + h : 2 * i + h + 1])
+
+        def difference(n):
+            t["diff", n] = work.tile([P, TILES, P], F32, name="diff", bufs=5)
+            nc.vector.tensor_tensor(out=t["diff", n][:], in0=t["vt", n][:],
+                                    in1=t["xkb", n // 2][:, :, P * (n % 2) : P * (n % 2 + 1)], op=ALU.subtract)
+
+        def statistics(n):
+            if n % 2 == 0:
+                t["stats", n // 2] = work.tile([P, 2 * TILES, 6], F32, name="stats")
+            for i in range(TILES):
+                nc.vector.bn_stats(out=t["stats", n // 2][:, TILES * (n % 2) + i, :],
+                                   in_=t["diff", n][:, i, :].rearrange("p (h d) -> p d h", h=2))
+
+        def deviation(m):
+            st = t["stats", m][:].rearrange("p i (h s) -> p (i h) s", h=2)
+            t["std", m] = work.tile([P, 4 * TILES], F32, name="std")
+            nc.scalar.activation(out=t["std", m][:], in_=st[:, :, 2], func=ACT.Sqrt, scale=1.0 / (HD - 1))
+            t["nmean", m] = work.tile([P, 4 * TILES], F32, name="nmean")
+            nc.scalar.activation(out=t["nmean", m][:], in_=st[:, :, 1], func=ACT.Copy, scale=-1.0)
+            t["stde", m] = work.tile([P, 4 * TILES], F32, name="stde")
+            nc.scalar.activation(out=t["stde", m][:], in_=t["std", m][:], func=ACT.Copy, bias=1e-8)
+
+        def deviation_inverse(m):
+            t["rs", m] = work.tile([P, 4 * TILES], F32, name="rs")
+            nc.vector.reciprocal(out=t["rs", m][:], in_=t["stde", m][:])
+
+        def shift(m):
+            t["nb", m] = work.tile([P, 4 * TILES], F32, name="nb")
+            eng = nc.gpsimd if m < UNITS // 2 - LAST else nc.vector
+            eng.tensor_tensor(out=t["nb", m][:], in0=t["nmean", m][:], in1=t["rs", m][:], op=ALU.mult)
+
+        def standardise(n):
+            dst = pair_tile("z", n, 2)
+            for i in range(TILES):
+                for h in range(2):
+                    cols = slice(HD * h, HD * (h + 1))
+                    q = 2 * TILES * (n % 2) + 2 * i + h
+                    nc.scalar.activation(out=dst[:, i, cols], in_=t["diff", n][:, i, cols], func=ACT.Identity,
+                                         scale=t["rs", n // 2][:, q : q + 1], bias=t["nb", n // 2][:, q : q + 1])
+
+        def pair_columns(m):
+            b, c = divmod(2 * m, CHUNKS)
+            return b, slice(P * c, P * (c + 2))
+
+        def target(m):
+            b, cols = pair_columns(m)
+            zw = work.tile([P, TILES, 2 * P], F32, name="zw", bufs=1)
+            nc.gpsimd.tensor_tensor(out=zw[:], in0=t["z", m][:],
+                                    in1=gamma[:, cols].unsqueeze(1).to_broadcast([P, TILES, 2 * P]), op=ALU.mult)
+            xv = work.tile([P, TILES, 2 * P], F32, name="xv", bufs=2)
+            nc.gpsimd.tensor_tensor(out=xv[:], in0=zw[:], in1=t["xkb", m][:], op=ALU.add)
+            nc.sync.dma_start(out=xv_hbm[b, :, :, cols], in_=xv[:])
+
+        def late_scale(n):
+            c = n % CHUNKS
+            t["zw", n] = work.tile([P, TILES, P], F32, name="zw_late", bufs=2)
+            nc.vector.tensor_tensor(out=t["zw", n][:], in0=t["z", n // 2][:, :, P * (n % 2) : P * (n % 2 + 1)],
+                                    in1=gamma[:, P * c : P * (c + 1)].unsqueeze(1).to_broadcast([P, TILES, P]), op=ALU.mult)
+
+        def late_target(n):
+            b, c = divmod(n, CHUNKS)
+            xv = work.tile([P, TILES, P], F32, name="xv_late", bufs=3)
+            nc.vector.tensor_tensor(out=xv[:], in0=t["zw", n][:],
+                                    in1=t["xkb", n // 2][:, :, P * (n % 2) : P * (n % 2 + 1)], op=ALU.add)
+            nc.sync.dma_start(out=xv_hbm[b, :, :, P * c : P * (c + 1)], in_=xv[:])
+
+        def late(n):
+            return UNITS - 2 * LAST <= n < UNITS
+
+        def store_key(m):
+            b, cols = pair_columns(m)
+            nc.sync.dma_start(out=xk_hbm[b, :, :, cols], in_=t["xk", m][:])
+
+        def live(n):
+            return 0 <= n < UNITS
+
+        def pair_done(n):
+            return live(n) and n % 2 == 1
+
+        for s in range(UNITS + 9):
+            if 1 <= s <= TILES:
+                nb, feeds = 1, [2 * s - 2, 2 * s - 1]
+            else:
+                nb, j = divmod(s + CHUNKS + 2, CHUNKS)
+                feeds = [j] if 2 <= nb < B else []
+            qb, qj = divmod(s + CHUNKS, CHUNKS)
+            quantising = {2: 0, 6: 1} if qb > 1 else {4: 0, 6: 1}
+
+            if live(s - 2):
+                sum_squares(s - 2)
+                rotate(s - 2)
+            if live(s - 3):
+                turn_value(s - 3)
+            if feeds:
+                if feeds[0] == 0:
+                    open_batch(nb)
+                bank = psum.tile([P, len(feeds), 2, P], F32, name="xt", tag="xt")
+                for k, j in enumerate(feeds):
+                    turn(bank[:, k], nb, j % TILES, j // TILES)
+
+            if live(s - 1):
+                value(s - 1)
+                rope_terms(s - 1)
+            if pair_done(s - 5):
+                deviation((s - 5) // 2)
+            if live(s - 2):
+                norm_floor(s - 2)
+            if live(s - 7):
+                standardise(s - 7)
+            if live(s - 3):
+                key_plus_bias(s - 3)
+            if live(s - 1):
+                squares(s - 1)
+            if qb < B and qj in quantising:
+                quantise(qb, quantising[qj])
+            if pair_done(s - 5):
+                deviation_inverse((s - 5) // 2)
+                shift((s - 5) // 2)
+            if live(s - 2):
+                norm_root(s - 2)
+            if live(s - 4):
+                statistics(s - 4)
+            if live(s - 2):
+                norm_inverse(s - 2)
+            if live(s - 3):
+                difference(s - 3)
+                key(s - 3)
+            for k, j in enumerate(feeds):
+                nc.scalar.copy(out=grouped_words(nb, j % TILES, j // TILES), in_=bank[:, k].rearrange("p u r -> p r u"))
+            if pair_done(s - 3):
+                store_key((s - 3) // 2)
+            if pair_done(s - 7) and not late(s - 7):
+                target((s - 7) // 2)
+            if late(s - 7):
+                late_scale(s - 7)
+            if late(s - 8):
+                late_target(s - 8)
+            if live(s):
+                project(s)

@@ -22,7 +22,9 @@ TILES = L // P
 CHUNKS = D // P
 UNITS = B * CHUNKS
 HALF = 4
-LAST = 2
+KINDS = "MMMMMMMMMMMMMADD"
+NA, NV = 2, 1
+NL, LAG = 1, 7
 
 
 def tile_tttwrapper_pa_kernel(tc, hidden_states, freqs_cis, wk_w_words, wk_w_scales, wk_b,
@@ -45,12 +47,12 @@ def tile_tttwrapper_pa_kernel(tc, hidden_states, freqs_cis, wk_w_words, wk_w_sca
         rows = keep.tile([P, P], BF16, name="rows")
         nc.vector.memset(rows[:], 0.0)
 
+        ident = keep.tile([P, P], F32, name="ident")
+        make_identity(nc, ident[:])
         freqs = keep.tile([P, TILES, HD], BF16, name="freqs")
         nc.scalar.dma_start(out=freqs[:], in_=freqs_cis.rearrange("(i p) j e -> p i (j e)", p=P))
-        nc.scalar.dma_start(out=rows[0:8, :], in_=wk_b.rearrange("(c m) -> c m", m=P))
-        nc.scalar.dma_start(out=rows[8:16, :], in_=wv_b.rearrange("(c m) -> c m", m=P))
-        nc.scalar.dma_start(out=rows[16:24, :], in_=ttt_norm_bias.rearrange("(c h) d -> c (h d)", h=2))
-        nc.scalar.dma_start(out=rows[24:32, :], in_=ttt_norm_weight.rearrange("(c h) d -> c (h d)", h=2))
+        nc.gpsimd.dma_start(out=rows[0:8, :], in_=wk_b.rearrange("(c m) -> c m", m=P))
+        nc.gpsimd.dma_start(out=rows[8:16, :], in_=wv_b.rearrange("(c m) -> c m", m=P))
 
         x = {}
 
@@ -77,15 +79,17 @@ def tile_tttwrapper_pa_kernel(tc, hidden_states, freqs_cis, wk_w_words, wk_w_sca
         load_scales("v", wv_w_scales)
         load_words("v", wv_w_words, 0)
         load_x(1)
+        beta_bf = keep.tile([P, D], BF16, name="beta_bf")
+        nc.sync.dma_start(out=beta_bf[:], in_=ttt_norm_bias.rearrange("h d -> (h d)").partition_broadcast(P))
         load_words("k", wk_w_words, 1)
         load_words("v", wv_w_words, 1)
+        gamma_bf = keep.tile([P, D], BF16, name="gamma_bf")
+        nc.sync.dma_start(out=gamma_bf[:], in_=ttt_norm_weight.rearrange("h d -> (h d)").partition_broadcast(P))
         load_x(2)
         load_x(3)
 
-        ident = keep.tile([P, P], F32, name="ident")
-        make_identity(nc, ident[:])
         ident_bf = keep.tile([P, P], BF16, name="ident_bf")
-        make_identity(nc, ident_bf[:])
+        nc.vector.tensor_copy(out=ident_bf[:], in_=ident[:])
         swap = keep.tile([P, P], F32, name="swap")
         for e in range(2):
             nc.vector.tensor_copy(out=swap[:, e::2], in_=ident[:, 1 - e :: 2])
@@ -127,50 +131,41 @@ def tile_tttwrapper_pa_kernel(tc, hidden_states, freqs_cis, wk_w_words, wk_w_sca
             nc.vector.quantize_mx(out=codes[b][:, g, :].bitcast(E5M2), scales=scales[b][:, g, :], in_=grouped[b][:, g, :])
 
         open_batch(0)
+        first_tags = (("u", 2), ("k", 2), ("u", 2), ("k", 2), ("v", 1), ("xt", 1), ("u", 2), ("k", 2))
         for i in range(TILES):
-            bank = psum.tile([P, PASSES, 2, P], F32, name="first_x", tag="u" if i < 2 else "k", bufs=2)
             for g in range(PASSES):
-                turn(bank[:, g], 0, i, g)
-            for g in range(PASSES):
-                if i % 2 == 0:
-                    nc.scalar.copy(out=grouped_words(0, i, g), in_=bank[:, g].rearrange("p u r -> p r u"))
+                tag, bufs = first_tags[PASSES * i + g]
+                bank = psum.tile([P, 2, P], F32, name="first_x", tag=tag, bufs=bufs)
+                turn(bank, 0, i, g)
+                if g == 0:
+                    nc.scalar.copy(out=grouped_words(0, i, g), in_=bank[:].rearrange("p u r -> p r u"))
                 else:
-                    nc.vector.tensor_copy(out=grouped_words(0, i, g), in_=bank[:, g].rearrange("p u r -> p r u"))
-            if i == 1:
-                rows_t = psum.tile([P, P], BF16, name="rows_t", tag="ss")
-                nc.tensor.transpose(rows_t[:], rows[:], ident_bf[:])
-                table_t = psum.tile([P, 2, L], BF16, name="table_t", tag="vt")
-                for cs in range(2):
-                    for t in range(TILES):
-                        nc.tensor.transpose(table_t[:, cs, P * t : P * (t + 1)], spread[:, cs, t, :], ident_bf[:])
+                    nc.vector.tensor_copy(out=grouped_words(0, i, g), in_=bank[:].rearrange("p u r -> p r u"))
+        table_t = psum.tile([P, 2, L], BF16, name="table_t", tag="vt")
+        for cs in range(2):
+            for i in range(TILES):
+                nc.tensor.transpose(table_t[:, cs, P * i : P * (i + 1)], spread[:, cs, i, :], ident_bf[:])
+        rows_t = psum.tile([P, P], BF16, name="rows_t", tag="ss")
+        nc.tensor.transpose(rows_t[:], rows[:], ident_bf[:])
         table = keep.tile([P, 2, L], BF16, name="table")
         nc.scalar.copy(out=table[:], in_=table_t[:])
-        columns = keep.tile([P, 3 * CHUNKS], F32, name="columns")
-        nc.scalar.copy(out=columns[:], in_=rows_t[:, 0 : 3 * CHUNKS])
+        columns = keep.tile([P, 2 * CHUNKS], F32, name="columns")
+        nc.scalar.copy(out=columns[:], in_=rows_t[:, 0 : 2 * CHUNKS])
         for g in range(PASSES):
             quantise(0, g)
-        bias_v = keep.tile([P, CHUNKS], F32, name="bias_v")
-        nc.vector.tensor_tensor(out=bias_v[:], in0=columns[:, CHUNKS : 2 * CHUNKS], in1=columns[:, 2 * CHUNKS :], op=ALU.add)
-
-        def spread_rows(first_row, name, tags):
-            wide = keep.tile([P, D], F32, name=name)
-            for half in range(2):
-                bank = psum.tile([P, HALF, P], F32, name="spread_" + name, tag=tags[half])
-                for c in range(HALF):
-                    r = first_row + HALF * half + c
-                    nc.tensor.matmul(bank[:, c, :], lhsT=ident_bf[:, r : r + 1].to_broadcast([P, P]), rhs=rows[:],
-                                     start=True, stop=True)
-                nc.scalar.copy(out=wide[:, HALF * P * half : HALF * P * (half + 1)], in_=bank[:].rearrange("p c m -> p (c m)"))
-            return wide
-
-        beta = spread_rows(2 * CHUNKS, "beta", ("v", "xt"))
-        gamma = spread_rows(3 * CHUNKS, "gamma", ("ss", "vt"))
+        beta = keep.tile([P, D], F32, name="beta")
+        nc.gpsimd.tensor_scalar(out=beta[:], in0=beta_bf[:], scalar1=1.0, scalar2=0.0, op0=ALU.mult, op1=ALU.add)
+        gamma = keep.tile([P, D], F32, name="gamma")
+        nc.gpsimd.tensor_scalar(out=gamma[:], in0=gamma_bf[:], scalar1=1.0, scalar2=0.0, op0=ALU.mult, op1=ALU.add)
 
         t = {}
 
-        def project(n):
+        def kind(n):
+            return KINDS[n // 2]
+
+        def project(kv, n):
             b, c = divmod(n, CHUNKS)
-            for kv in ("k", "v"):
+            if True:
                 t[kv, n] = psum.tile([P, L], F32, name="proj_" + kv, tag=kv, bufs=2 if kv == "k" else 1)
                 for g in range(PASSES):
                     nc.tensor.matmul_mx(
@@ -194,7 +189,8 @@ def tile_tttwrapper_pa_kernel(tc, hidden_states, freqs_cis, wk_w_words, wk_w_sca
         def value(n):
             c = n % CHUNKS
             t["v0", n] = work.tile([P, L], F32, name="v0", bufs=4)
-            nc.scalar.activation(out=t["v0", n][:], in_=t["v", n][:], func=ACT.Identity, bias=bias_v[:, c : c + 1])
+            nc.scalar.activation(out=t["v0", n][:], in_=t["v", n][:], func=ACT.Identity,
+                                 bias=columns[:, CHUNKS + c : CHUNKS + c + 1])
 
         def sum_squares(n):
             t["ss", n] = psum.tile([P, 2 * TILES], F32, name="ss", tag="ss")
@@ -218,11 +214,11 @@ def tile_tttwrapper_pa_kernel(tc, hidden_states, freqs_cis, wk_w_words, wk_w_sca
 
         def norm_floor(n):
             t["ssm", n] = work.tile([P, 2 * TILES], F32, name="ssm")
-            nc.vector.tensor_scalar(out=t["ssm", n][:], in0=t["ss", n][:], scalar1=1e-24, scalar2=None, op0=ALU.max)
+            nc.scalar.activation(out=t["ssm", n][:], in_=t["ss", n][:], func=ACT.Relu, bias=-1e-24)
 
         def norm_root(n):
             t["nrm", n] = work.tile([P, 2 * TILES], F32, name="nrm")
-            nc.scalar.activation(out=t["nrm", n][:], in_=t["ssm", n][:], func=ACT.Sqrt)
+            nc.scalar.activation(out=t["nrm", n][:], in_=t["ssm", n][:], func=ACT.Sqrt, bias=1e-24)
 
         def norm_inverse(n):
             t["r", n] = work.tile([P, 2 * TILES], F32, name="r")
@@ -233,63 +229,82 @@ def tile_tttwrapper_pa_kernel(tc, hidden_states, freqs_cis, wk_w_words, wk_w_sca
                 t[kind, n // 2] = work.tile([P, TILES, 2 * P], F32, name=kind, bufs=bufs)
             return t[kind, n // 2][:, :, P * (n % 2) : P * (n % 2 + 1)]
 
+        def wide_tiles(n):
+            return NV if kind(n) == "M" else NL
+
+        def pooled_tiles(n):
+            return TILES - NA if kind(n) == "M" else 0
+
         def key_plus_bias(n):
             c = n % CHUNKS
             dst = pair_tile("xkb", n, 4)
-            for i in range(TILES):
+            for i in range(pooled_tiles(n), TILES):
                 for h in range(2):
                     cols = slice(HD * h, HD * (h + 1))
                     nc.vector.scalar_tensor_tensor(out=dst[:, i, cols], in0=t["u", n][:, i, cols],
                                                    scalar=t["r", n][:, 2 * i + h : 2 * i + h + 1],
-                                                   in1=beta[:, P * c + HD * h : P * c + HD * (h + 1)],
+                                                   in1=beta_bf[:, P * c + HD * h : P * c + HD * (h + 1)],
                                                    op0=ALU.mult, op1=ALU.add)
 
         def key(n):
-            dst = pair_tile("xk", n, 3)
-            for i in range(TILES):
+            dst = pair_tile("xk", n, 4)
+            for i in range(wide_tiles(n), TILES):
                 for h in range(2):
                     cols = slice(HD * h, HD * (h + 1))
                     nc.scalar.activation(out=dst[:, i, cols], in_=t["u", n][:, i, cols], func=ACT.Copy,
                                          scale=t["r", n][:, 2 * i + h : 2 * i + h + 1])
 
+        def key_wide(n):
+            k = wide_tiles(n)
+            dst = t["xk", n // 2][:, 0:k, P * (n % 2) : P * (n % 2 + 1)]
+            for_heads = "p i (h d) -> p i h d"
+            nc.vector.tensor_tensor(out=dst.rearrange(for_heads, h=2), in0=t["u", n][:, 0:k, :].rearrange(for_heads, h=2),
+                                    in1=t["r", n][:, 0 : 2 * k].rearrange("p (i h) -> p i h", h=2).unsqueeze(3).to_broadcast([P, k, 2, HD]),
+                                    op=ALU.mult)
+
+        def add_beta(m):
+            b, cols = pair_columns(m)
+            k = pooled_tiles(2 * m)
+            nc.gpsimd.tensor_tensor(out=t["xkb", m][:, 0:k, :], in0=t["xk", m][:, 0:k, :],
+                                    in1=beta[:, cols].unsqueeze(1).to_broadcast([P, k, 2 * P]), op=ALU.add)
+
         def difference(n):
             t["diff", n] = work.tile([P, TILES, P], F32, name="diff", bufs=5)
             nc.vector.tensor_tensor(out=t["diff", n][:], in0=t["vt", n][:],
-                                    in1=t["xkb", n // 2][:, :, P * (n % 2) : P * (n % 2 + 1)], op=ALU.subtract)
+                                    in1=t["xk", n // 2][:, :, P * (n % 2) : P * (n % 2 + 1)], op=ALU.subtract)
 
         def statistics(n):
-            if n % 2 == 0:
-                t["stats", n // 2] = work.tile([P, 2 * TILES, 6], F32, name="stats")
+            t["stats", n] = work.tile([P, TILES, 6], F32, name="stats", bufs=4)
             for i in range(TILES):
-                nc.vector.bn_stats(out=t["stats", n // 2][:, TILES * (n % 2) + i, :],
-                                   in_=t["diff", n][:, i, :].rearrange("p (h d) -> p d h", h=2))
+                nc.vector.bn_stats(out=t["stats", n][:, i, :], in_=t["diff", n][:, i, :].rearrange("p (h d) -> p d h", h=2))
 
-        def deviation(m):
-            st = t["stats", m][:].rearrange("p i (h s) -> p (i h) s", h=2)
-            t["std", m] = work.tile([P, 4 * TILES], F32, name="std")
-            nc.scalar.activation(out=t["std", m][:], in_=st[:, :, 2], func=ACT.Sqrt, scale=1.0 / (HD - 1))
-            t["nmean", m] = work.tile([P, 4 * TILES], F32, name="nmean")
-            nc.scalar.activation(out=t["nmean", m][:], in_=st[:, :, 1], func=ACT.Copy, scale=-1.0)
-            t["stde", m] = work.tile([P, 4 * TILES], F32, name="stde")
-            nc.scalar.activation(out=t["stde", m][:], in_=t["std", m][:], func=ACT.Copy, bias=1e-8)
+        def by_head(n):
+            return t["stats", n][:].rearrange("p i (h s) -> p (i h) s", h=2)
 
-        def deviation_inverse(m):
-            t["rs", m] = work.tile([P, 4 * TILES], F32, name="rs")
-            nc.vector.reciprocal(out=t["rs", m][:], in_=t["stde", m][:])
+        def deviation(n):
+            std = work.tile([P, 2 * TILES], F32, name="std")
+            nc.scalar.activation(out=std[:], in_=by_head(n)[:, :, 2], func=ACT.Sqrt, scale=1.0 / (HD - 1))
+            t["std", n] = std
 
-        def shift(m):
-            t["nb", m] = work.tile([P, 4 * TILES], F32, name="nb")
-            eng = nc.gpsimd if m < UNITS // 2 - LAST else nc.vector
-            eng.tensor_tensor(out=t["nb", m][:], in0=t["nmean", m][:], in1=t["rs", m][:], op=ALU.mult)
+        def deviation_floor(n):
+            t["stde", n] = work.tile([P, 2 * TILES], F32, name="stde")
+            nc.scalar.activation(out=t["stde", n][:], in_=t["std", n][:], func=ACT.Copy, bias=1e-8)
+
+        def deviation_inverse(n):
+            nc.vector.reciprocal(out=by_head(n)[:, :, 0], in_=t["stde", n][:])
+
+        def shift(n):
+            t["nb", n] = work.tile([P, 2 * TILES], F32, name="nb")
+            nc.vector.tensor_reduce(out=t["nb", n][:], in_=by_head(n)[:, :, 0:2], axis=mybir.AxisListType.X, op=ALU.mult, negate=True)
 
         def standardise(n):
-            dst = pair_tile("z", n, 2)
+            dst = pair_tile("z", n, 3)
             for i in range(TILES):
                 for h in range(2):
                     cols = slice(HD * h, HD * (h + 1))
-                    q = 2 * TILES * (n % 2) + 2 * i + h
+                    q = 2 * i + h
                     nc.scalar.activation(out=dst[:, i, cols], in_=t["diff", n][:, i, cols], func=ACT.Identity,
-                                         scale=t["rs", n // 2][:, q : q + 1], bias=t["nb", n // 2][:, q : q + 1])
+                                         scale=by_head(n)[:, q, 0:1], bias=t["nb", n][:, q : q + 1])
 
         def pair_columns(m):
             b, c = divmod(2 * m, CHUNKS)
@@ -297,9 +312,11 @@ def tile_tttwrapper_pa_kernel(tc, hidden_states, freqs_cis, wk_w_words, wk_w_sca
 
         def target(m):
             b, cols = pair_columns(m)
-            zw = work.tile([P, TILES, 2 * P], F32, name="zw", bufs=1)
+            zw = work.tile([P, TILES, 2 * P], F32, name="zw", bufs=2)
             nc.gpsimd.tensor_tensor(out=zw[:], in0=t["z", m][:],
                                     in1=gamma[:, cols].unsqueeze(1).to_broadcast([P, TILES, 2 * P]), op=ALU.mult)
+            if pooled_tiles(2 * m + 2):
+                add_beta(m + 1)
             xv = work.tile([P, TILES, 2 * P], F32, name="xv", bufs=2)
             nc.gpsimd.tensor_tensor(out=xv[:], in0=zw[:], in1=t["xkb", m][:], op=ALU.add)
             nc.sync.dma_start(out=xv_hbm[b, :, :, cols], in_=xv[:])
@@ -312,13 +329,16 @@ def tile_tttwrapper_pa_kernel(tc, hidden_states, freqs_cis, wk_w_words, wk_w_sca
 
         def late_target(n):
             b, c = divmod(n, CHUNKS)
-            xv = work.tile([P, TILES, P], F32, name="xv_late", bufs=3)
+            xv = work.tile([P, TILES, P], F32, name="xv_late", bufs=4)
             nc.vector.tensor_tensor(out=xv[:], in0=t["zw", n][:],
                                     in1=t["xkb", n // 2][:, :, P * (n % 2) : P * (n % 2 + 1)], op=ALU.add)
             nc.sync.dma_start(out=xv_hbm[b, :, :, P * c : P * (c + 1)], in_=xv[:])
 
         def late(n):
-            return UNITS - 2 * LAST <= n < UNITS
+            return live(n) and kind(n) == "D"
+
+        def early(n):
+            return live(n) and kind(n) != "D"
 
         def store_key(m):
             b, cols = pair_columns(m)
@@ -330,63 +350,76 @@ def tile_tttwrapper_pa_kernel(tc, hidden_states, freqs_cis, wk_w_words, wk_w_sca
         def pair_done(n):
             return live(n) and n % 2 == 1
 
-        for s in range(UNITS + 9):
+        fed = []
+        for s in range(UNITS + LAG + 1):
             if 1 <= s <= TILES:
                 nb, feeds = 1, [2 * s - 2, 2 * s - 1]
             else:
                 nb, j = divmod(s + CHUNKS + 2, CHUNKS)
                 feeds = [j] if 2 <= nb < B else []
             qb, qj = divmod(s + CHUNKS, CHUNKS)
-            quantising = {2: 0, 6: 1} if qb > 1 else {4: 0, 6: 1}
 
+            if live(s):
+                project("k", s)
             if live(s - 2):
                 sum_squares(s - 2)
-                rotate(s - 2)
+            if live(s - 1):
+                value(s - 1)
+                rope_terms(s - 1)
+            if live(s - 5):
+                deviation(s - 5)
+            if live(s - 3):
+                key(s - 3)
+            if live(s):
+                project("v", s)
             if live(s - 3):
                 turn_value(s - 3)
+            if live(s - 2):
+                rotate(s - 2)
+            if live(s - 5):
+                deviation_floor(s - 5)
+            if live(s - 1):
+                squares(s - 1)
+            if live(s - 2):
+                norm_floor(s - 2)
+            for k, (fb, j) in enumerate(fed):
+                nc.scalar.copy(out=grouped_words(fb, j % TILES, j // TILES), in_=bank[:, k].rearrange("p u r -> p r u"))
+            fed = [(nb, j) for j in feeds]
             if feeds:
                 if feeds[0] == 0:
                     open_batch(nb)
                 bank = psum.tile([P, len(feeds), 2, P], F32, name="xt", tag="xt")
                 for k, j in enumerate(feeds):
                     turn(bank[:, k], nb, j % TILES, j // TILES)
-
-            if live(s - 1):
-                value(s - 1)
-                rope_terms(s - 1)
-            if pair_done(s - 5):
-                deviation((s - 5) // 2)
-            if live(s - 2):
-                norm_floor(s - 2)
-            if live(s - 7):
-                standardise(s - 7)
-            if live(s - 3):
-                key_plus_bias(s - 3)
-            if live(s - 1):
-                squares(s - 1)
-            if qb < B and qj in quantising:
-                quantise(qb, quantising[qj])
-            if pair_done(s - 5):
-                deviation_inverse((s - 5) // 2)
-                shift((s - 5) // 2)
             if live(s - 2):
                 norm_root(s - 2)
+            if live(s - 6):
+                standardise(s - 6)
             if live(s - 4):
                 statistics(s - 4)
-            if live(s - 2):
-                norm_inverse(s - 2)
+            if live(s - 3):
+                if wide_tiles(s - 3):
+                    key_wide(s - 3)
+                key_plus_bias(s - 3)
+            if live(s - 5):
+                deviation_inverse(s - 5)
             if live(s - 3):
                 difference(s - 3)
-                key(s - 3)
-            for k, j in enumerate(feeds):
-                nc.scalar.copy(out=grouped_words(nb, j % TILES, j // TILES), in_=bank[:, k].rearrange("p u r -> p r u"))
+            if live(s - 5):
+                shift(s - 5)
+            if live(s - 2):
+                norm_inverse(s - 2)
+            if qb < B and qj == 6:
+                nc.vector.quantize_mx(out=codes[qb][:].rearrange("p g n -> p (g n)").bitcast(E5M2),
+                                      scales=scales[qb][:].rearrange("p g n -> p (g n)"),
+                                      in_=grouped[qb][:].rearrange("p g n -> p (g n)"))
             if pair_done(s - 3):
                 store_key((s - 3) // 2)
-            if pair_done(s - 7) and not late(s - 7):
-                target((s - 7) // 2)
-            if late(s - 7):
-                late_scale(s - 7)
-            if late(s - 8):
-                late_target(s - 8)
-            if live(s):
-                project(s)
+            if pair_done(s - 6) and early(s - 6):
+                target((s - 6) // 2)
+            if s == 4 and pooled_tiles(0):
+                add_beta(0)
+            if late(s - LAG):
+                late_scale(s - LAG)
+            if late(s - LAG - 1):
+                late_target(s - LAG - 1)

@@ -23,8 +23,8 @@ CHUNKS = D // P
 UNITS = B * CHUNKS
 HALF = 4
 KINDS = "MMMMMMMMMMMMMADD"
-NA, NV = 2, 1
-NL, LAG = 1, 7
+NA, NV = 1, 2
+NL, LAG = 1, 6
 
 
 def tile_tttwrapper_pa_kernel(tc, hidden_states, freqs_cis, wk_w_words, wk_w_scales, wk_b,
@@ -365,19 +365,22 @@ def tile_tttwrapper_pa_kernel(tc, hidden_states, freqs_cis, wk_w_words, wk_w_sca
                 sum_squares(s - 2)
             if live(s - 1):
                 value(s - 1)
+            if live(s - 1):
                 rope_terms(s - 1)
             if live(s - 5):
-                deviation(s - 5)
+                deviation_inverse(s - 5)
             if live(s - 3):
                 key(s - 3)
+            if live(s - 4):
+                statistics(s - 4)
+            if live(s - 5):
+                shift(s - 5)
             if live(s):
                 project("v", s)
             if live(s - 3):
                 turn_value(s - 3)
             if live(s - 2):
                 rotate(s - 2)
-            if live(s - 5):
-                deviation_floor(s - 5)
             if live(s - 1):
                 squares(s - 1)
             if live(s - 2):
@@ -391,22 +394,20 @@ def tile_tttwrapper_pa_kernel(tc, hidden_states, freqs_cis, wk_w_words, wk_w_sca
                 bank = psum.tile([P, len(feeds), 2, P], F32, name="xt", tag="xt")
                 for k, j in enumerate(feeds):
                     turn(bank[:, k], nb, j % TILES, j // TILES)
+            if live(s - 4):
+                deviation(s - 4)
             if live(s - 2):
                 norm_root(s - 2)
-            if live(s - 6):
-                standardise(s - 6)
+            if live(s - 5):
+                standardise(s - 5)
             if live(s - 4):
-                statistics(s - 4)
+                deviation_floor(s - 4)
             if live(s - 3):
                 if wide_tiles(s - 3):
                     key_wide(s - 3)
                 key_plus_bias(s - 3)
-            if live(s - 5):
-                deviation_inverse(s - 5)
             if live(s - 3):
                 difference(s - 3)
-            if live(s - 5):
-                shift(s - 5)
             if live(s - 2):
                 norm_inverse(s - 2)
             if qb < B and qj == 6:
@@ -415,8 +416,8 @@ def tile_tttwrapper_pa_kernel(tc, hidden_states, freqs_cis, wk_w_words, wk_w_sca
                                       in_=grouped[qb][:].rearrange("p g n -> p (g n)"))
             if pair_done(s - 3):
                 store_key((s - 3) // 2)
-            if pair_done(s - 6) and early(s - 6):
-                target((s - 6) // 2)
+            if pair_done(s - 5) and early(s - 5):
+                target((s - 5) // 2)
             if s == 4 and pooled_tiles(0):
                 add_beta(0)
             if late(s - LAG):

@@ -3,7 +3,7 @@ from contextlib import ExitStack
 import concourse.mybir as mybir
 from concourse.masks import make_identity
 
-B, L, D, H, HD = 4, 512, 1024, 16, 64
+B, L, D, HD = 4, 512, 1024, 64
 FLOPS = 2 * 2 * B * L * D * D
 
 F32 = mybir.dt.float32
@@ -21,10 +21,13 @@ PASSES = D // 512
 TILES = L // P
 CHUNKS = D // P
 UNITS = B * CHUNKS
-HALF = 4
-KINDS = "MMMMMMMMMMMMMADD"
-NA, NV = 1, 2
-NL, LAG = 1, 6
+HEADS = 2 * TILES
+LOAD_CHUNKS = CHUNKS // 2
+NORM_FLOOR = 1e-12
+STD_EPS = 1e-8
+VECTOR_UNITS = 4
+DEPTH = 7
+QUANTISE_STEP = 6
 
 
 def tile_tttwrapper_pa_kernel(tc, hidden_states, freqs_cis, wk_w_words, wk_w_scales, wk_b,
@@ -40,38 +43,47 @@ def tile_tttwrapper_pa_kernel(tc, hidden_states, freqs_cis, wk_w_words, wk_w_sca
         psum = ctx.enter_context(tc.psum_pool(name="psum", bufs=1))
         ctx.enter_context(tc.manual_schedule())
 
-        planes = {}
+        banks = {"k": 2, "v": 1, "rot": 2, "vt": 1, "xt": 1, "side": 1}
+
+        def bank_tile(shape, dtype, name, tag):
+            return psum.tile(shape, dtype, name=name, tag=tag, bufs=banks[tag])
+
+        w_scales = {}
         for kv in ("k", "v"):
-            planes[kv] = keep.tile([P, PASSES, D], U8, name="plane_" + kv, align_bytes=64)
-            nc.vector.memset(planes[kv][:].rearrange("p g n -> p (g n)").bitcast(I32), 0)
-        rows = keep.tile([P, P], BF16, name="rows")
-        nc.vector.memset(rows[:], 0.0)
+            w_scales[kv] = keep.tile([P, PASSES, D], U8, name="w_scales_" + kv, align_bytes=64)
+            nc.vector.memset(w_scales[kv][:].rearrange("p g n -> p (g n)").bitcast(I32), 0)
+        bias_rows = keep.tile([P, P], BF16, name="bias_rows")
+        nc.vector.memset(bias_rows[:], 0.0)
 
         ident = keep.tile([P, P], F32, name="ident")
         make_identity(nc, ident[:])
         freqs = keep.tile([P, TILES, HD], BF16, name="freqs")
         nc.scalar.dma_start(out=freqs[:], in_=freqs_cis.rearrange("(i p) j e -> p i (j e)", p=P))
-        nc.gpsimd.dma_start(out=rows[0:8, :], in_=wk_b.rearrange("(c m) -> c m", m=P))
-        nc.gpsimd.dma_start(out=rows[8:16, :], in_=wv_b.rearrange("(c m) -> c m", m=P))
+        nc.gpsimd.dma_start(out=bias_rows[0:CHUNKS, :], in_=wk_b.rearrange("(c m) -> c m", m=P))
+        nc.gpsimd.dma_start(out=bias_rows[CHUNKS : 2 * CHUNKS, :], in_=wv_b.rearrange("(c m) -> c m", m=P))
 
-        x = {}
+        x, w_words = {}, {}
 
         def load_x(b):
             for i in range(TILES):
                 x[b, i] = keep.tile([P, D], BF16, name="x_%d_%d" % (b, i))
                 nc.sync.dma_start(out=x[b, i][:], in_=hidden_states[b, P * i : P * (i + 1), :])
 
-        words = {}
-
         def load_words(kv, src, half):
-            words[kv, half] = keep.tile([P, PASSES, D], U8, name="words_%s_%d" % (kv, half), align_bytes=64)
-            nc.sync.dma_start(out=words[kv, half][:].bitcast(I32),
-                              in_=src[:, :, D * half : D * (half + 1)].rearrange("g p n -> p g n").bitcast(I32))
+            width = 2 * P * LOAD_CHUNKS
+            w_words[kv, half] = keep.tile([P, PASSES, width], U8, name="w_words_%s_%d" % (kv, half), align_bytes=64)
+            nc.sync.dma_start(out=w_words[kv, half][:].bitcast(I32),
+                              in_=src[:, :, width * half : width * (half + 1)].rearrange("g p n -> p g n").bitcast(I32))
 
         def load_scales(kv, src):
-            for q in range(4):
-                nc.sync.dma_start(out=planes[kv][32 * q : 32 * q + 4, :, :].bitcast(I32),
-                                  in_=src[:, 4 * q : 4 * q + 4, :].rearrange("g r n -> r g n").bitcast(I32))
+            for quad in range(4):
+                nc.sync.dma_start(out=w_scales[kv][32 * quad : 32 * quad + 4, :, :].bitcast(I32),
+                                  in_=src[:, 4 * quad : 4 * quad + 4, :].rearrange("g r n -> r g n").bitcast(I32))
+
+        def load_on_all_partitions(src, name):
+            wide = keep.tile([P, D], BF16, name=name)
+            nc.sync.dma_start(out=wide[:], in_=src.rearrange("h d -> (h d)").partition_broadcast(P))
+            return wide
 
         load_x(0)
         load_words("k", wk_w_words, 0)
@@ -79,12 +91,10 @@ def tile_tttwrapper_pa_kernel(tc, hidden_states, freqs_cis, wk_w_words, wk_w_sca
         load_scales("v", wv_w_scales)
         load_words("v", wv_w_words, 0)
         load_x(1)
-        beta_bf = keep.tile([P, D], BF16, name="beta_bf")
-        nc.sync.dma_start(out=beta_bf[:], in_=ttt_norm_bias.rearrange("h d -> (h d)").partition_broadcast(P))
+        beta_bf = load_on_all_partitions(ttt_norm_bias, "beta_bf")
         load_words("k", wk_w_words, 1)
         load_words("v", wv_w_words, 1)
-        gamma_bf = keep.tile([P, D], BF16, name="gamma_bf")
-        nc.sync.dma_start(out=gamma_bf[:], in_=ttt_norm_weight.rearrange("h d -> (h d)").partition_broadcast(P))
+        gamma_bf = load_on_all_partitions(ttt_norm_weight, "gamma_bf")
         load_x(2)
         load_x(3)
 
@@ -101,271 +111,246 @@ def tile_tttwrapper_pa_kernel(tc, hidden_states, freqs_cis, wk_w_words, wk_w_sca
         nc.vector.memset(sign[:, 0:1], 1.0)
         nc.vector.memset(sign[:, 1:2], -1.0)
 
-        spread = keep.tile([P, 2, TILES, P], BF16, name="spread")
-        pairs = freqs[:].rearrange("p i (j e) -> p i j e", e=2)
+        rope_rows = keep.tile([P, 2, TILES, P], BF16, name="rope_rows")
+        cos_sin = freqs[:].rearrange("p i (j e) -> p i j e", e=2)
+        pair_shape = [P, TILES, HD // 2, 2]
         for h in range(2):
             cols = slice(HD * h, HD * (h + 1))
-            nc.vector.tensor_copy(out=spread[:, 0, :, cols].rearrange("p i (j e) -> p i j e", e=2),
-                                  in_=pairs[:, :, :, 0:1].to_broadcast([P, TILES, HD // 2, 2]))
-            nc.vector.tensor_tensor(out=spread[:, 1, :, cols].rearrange("p i (j e) -> p i j e", e=2),
-                                    in0=pairs[:, :, :, 1:2].to_broadcast([P, TILES, HD // 2, 2]),
-                                    in1=sign[:].unsqueeze(1).unsqueeze(1).to_broadcast([P, TILES, HD // 2, 2]),
-                                    op=ALU.mult)
+            nc.vector.tensor_copy(out=rope_rows[:, 0, :, cols].rearrange("p i (j e) -> p i j e", e=2),
+                                  in_=cos_sin[:, :, :, 0:1].to_broadcast(pair_shape))
+            nc.vector.tensor_tensor(out=rope_rows[:, 1, :, cols].rearrange("p i (j e) -> p i j e", e=2),
+                                    in0=cos_sin[:, :, :, 1:2].to_broadcast(pair_shape),
+                                    in1=sign[:].unsqueeze(1).unsqueeze(1).to_broadcast(pair_shape), op=ALU.mult)
 
-        grouped, codes, scales = {}, {}, {}
+        grouped, x_codes, x_scales = {}, {}, {}
 
         def open_batch(b):
             grouped[b] = work.tile([P, PASSES, 4 * L], BF16, name="grouped", bufs=2, align_bytes=64)
-            codes[b] = work.tile([P, PASSES, L], U32, name="codes", bufs=2, align_bytes=64)
-            scales[b] = work.tile([P, PASSES, L], U8, name="scales", bufs=2, align_bytes=64)
+            x_codes[b] = work.tile([P, PASSES, L], U32, name="x_codes", bufs=2, align_bytes=64)
+            x_scales[b] = work.tile([P, PASSES, L], U8, name="x_scales", bufs=2, align_bytes=64)
 
-        def turn(bank, b, i, g):
-            w = x[b, i][:].bitcast(F32)
+        def transpose_piece(dst, b, i, g):
+            x_words = x[b, i][:].bitcast(F32)
             for u in range(2):
-                nc.tensor.transpose(bank[:, u, :], w[:, 256 * g + u : 256 * (g + 1) : 2], ident[:])
+                nc.tensor.transpose(dst[:, u, :], x_words[:, 256 * g + u : 256 * (g + 1) : 2], ident[:])
 
         def grouped_words(b, i, g):
             return grouped[b][:, g, 4 * P * i : 4 * P * (i + 1)].bitcast(F32).rearrange("p (r u) -> p r u", u=2)
 
-        def quantise(b, g):
-            nc.vector.quantize_mx(out=codes[b][:, g, :].bitcast(E5M2), scales=scales[b][:, g, :], in_=grouped[b][:, g, :])
-
         open_batch(0)
-        first_tags = (("u", 2), ("k", 2), ("u", 2), ("k", 2), ("v", 1), ("xt", 1), ("u", 2), ("k", 2))
+        first_tags = ("rot", "k", "rot", "k", "v", "xt", "rot", "k")
         for i in range(TILES):
             for g in range(PASSES):
-                tag, bufs = first_tags[PASSES * i + g]
-                bank = psum.tile([P, 2, P], F32, name="first_x", tag=tag, bufs=bufs)
-                turn(bank, 0, i, g)
+                piece = bank_tile([P, 2, P], F32, "first_piece", first_tags[PASSES * i + g])
+                transpose_piece(piece, 0, i, g)
                 if g == 0:
-                    nc.scalar.copy(out=grouped_words(0, i, g), in_=bank[:].rearrange("p u r -> p r u"))
+                    nc.scalar.copy(out=grouped_words(0, i, g), in_=piece[:].rearrange("p u r -> p r u"))
                 else:
-                    nc.vector.tensor_copy(out=grouped_words(0, i, g), in_=bank[:].rearrange("p u r -> p r u"))
-        table_t = psum.tile([P, 2, L], BF16, name="table_t", tag="vt")
+                    nc.vector.tensor_copy(out=grouped_words(0, i, g), in_=piece[:].rearrange("p u r -> p r u"))
+        rope_t = bank_tile([P, 2, L], BF16, "rope_t", "vt")
         for cs in range(2):
             for i in range(TILES):
-                nc.tensor.transpose(table_t[:, cs, P * i : P * (i + 1)], spread[:, cs, i, :], ident_bf[:])
-        rows_t = psum.tile([P, P], BF16, name="rows_t", tag="ss")
-        nc.tensor.transpose(rows_t[:], rows[:], ident_bf[:])
-        table = keep.tile([P, 2, L], BF16, name="table")
-        nc.scalar.copy(out=table[:], in_=table_t[:])
-        columns = keep.tile([P, 2 * CHUNKS], F32, name="columns")
-        nc.scalar.copy(out=columns[:], in_=rows_t[:, 0 : 2 * CHUNKS])
+                nc.tensor.transpose(rope_t[:, cs, P * i : P * (i + 1)], rope_rows[:, cs, i, :], ident_bf[:])
+        bias_t = bank_tile([P, P], BF16, "bias_t", "side")
+        nc.tensor.transpose(bias_t[:], bias_rows[:], ident_bf[:])
+        rope = keep.tile([P, 2, L], BF16, name="rope")
+        nc.scalar.copy(out=rope[:], in_=rope_t[:])
+        bias = keep.tile([P, 2 * CHUNKS], F32, name="bias")
+        nc.scalar.copy(out=bias[:], in_=bias_t[:, 0 : 2 * CHUNKS])
         for g in range(PASSES):
-            quantise(0, g)
-        beta = keep.tile([P, D], F32, name="beta")
-        nc.gpsimd.tensor_scalar(out=beta[:], in0=beta_bf[:], scalar1=1.0, scalar2=0.0, op0=ALU.mult, op1=ALU.add)
+            nc.vector.quantize_mx(out=x_codes[0][:, g, :].bitcast(E5M2), scales=x_scales[0][:, g, :], in_=grouped[0][:, g, :])
         gamma = keep.tile([P, D], F32, name="gamma")
         nc.gpsimd.tensor_scalar(out=gamma[:], in0=gamma_bf[:], scalar1=1.0, scalar2=0.0, op0=ALU.mult, op1=ALU.add)
 
+        def quantise(b):
+            nc.vector.quantize_mx(out=x_codes[b][:].rearrange("p g n -> p (g n)").bitcast(E5M2),
+                                  scales=x_scales[b][:].rearrange("p g n -> p (g n)"),
+                                  in_=grouped[b][:].rearrange("p g n -> p (g n)"))
+
+        def pieces_of_step(s):
+            if 1 <= s <= TILES:
+                b, numbers = 1, [2 * s - 2, 2 * s - 1]
+            else:
+                b, j = divmod(s + CHUNKS + 2, CHUNKS)
+                numbers = [j] if 2 <= b < B else []
+            return [(b, j % TILES, j // TILES) for j in numbers]
+
         t = {}
 
-        def kind(n):
-            return KINDS[n // 2]
+        def chunk_cols(n):
+            c = n % CHUNKS
+            return slice(P * c, P * (c + 1))
+
+        def per_head():
+            return [(i, slice(HD * h, HD * (h + 1)), 2 * i + h) for i in range(TILES) for h in range(2)]
+
+        def half_of_pair(kind, n):
+            return t[kind, n // 2][:, :, P * (n % 2) : P * (n % 2 + 1)]
+
+        def open_pair(kind, n, bufs):
+            if n % 2 == 0:
+                t[kind, n // 2] = work.tile([P, TILES, 2 * P], F32, name=kind, bufs=bufs)
+            return half_of_pair(kind, n)
+
+        def side_bank(s):
+            if ("side", s) not in t:
+                t["side", s] = bank_tile([P, 3, P], F32, "side", "side")
+            return t["side", s]
 
         def project(kv, n):
             b, c = divmod(n, CHUNKS)
-            if True:
-                t[kv, n] = psum.tile([P, L], F32, name="proj_" + kv, tag=kv, bufs=2 if kv == "k" else 1)
-                for g in range(PASSES):
-                    nc.tensor.matmul_mx(
-                        out=t[kv, n][:],
-                        lhsT=words[kv, c // HALF][:, g, 2 * P * (c % HALF) : 2 * P * (c % HALF + 1)].bitcast(E2M1),
-                        lhsT_scale=planes[kv][:, g, P * c : P * (c + 1)],
-                        rhs=codes[b][:, g, :].bitcast(E5M2), rhs_scale=scales[b][:, g, :],
-                        start=(g == 0), stop=(g == PASSES - 1))
+            half, c_in = divmod(c, LOAD_CHUNKS)
+            t[kv, n] = bank_tile([P, L], F32, "proj_" + kv, kv)
+            for g in range(PASSES):
+                nc.tensor.matmul_mx(out=t[kv, n][:],
+                                    lhsT=w_words[kv, half][:, g, 2 * P * c_in : 2 * P * (c_in + 1)].bitcast(E2M1),
+                                    lhsT_scale=w_scales[kv][:, g, chunk_cols(n)],
+                                    rhs=x_codes[b][:, g, :].bitcast(E5M2), rhs_scale=x_scales[b][:, g, :],
+                                    start=(g == 0), stop=(g == PASSES - 1))
+
+        def value(n):
+            c = CHUNKS + n % CHUNKS
+            t["v0", n] = work.tile([P, L], F32, name="v0", bufs=4)
+            nc.scalar.activation(out=t["v0", n][:], in_=t["v", n][:], func=ACT.Identity, bias=bias[:, c : c + 1])
 
         def rope_terms(n):
             c = n % CHUNKS
             t["terms", n] = work.tile([P, 2, L], F32, name="terms")
             nc.vector.scalar_tensor_tensor(out=t["terms", n][:], in0=t["k", n][:].unsqueeze(1).to_broadcast([P, 2, L]),
-                                           scalar=columns[:, c : c + 1], in1=table[:], op0=ALU.add, op1=ALU.mult)
+                                           scalar=bias[:, c : c + 1], in1=rope[:], op0=ALU.add, op1=ALU.mult)
 
         def squares(n):
             c = n % CHUNKS
             t["sq", n] = work.tile([P, L], F32, name="sq")
-            nc.scalar.activation(out=t["sq", n][:], in_=t["k", n][:], func=ACT.Square, bias=columns[:, c : c + 1])
+            nc.scalar.activation(out=t["sq", n][:], in_=t["k", n][:], func=ACT.Square, bias=bias[:, c : c + 1])
 
-        def value(n):
-            c = n % CHUNKS
-            t["v0", n] = work.tile([P, L], F32, name="v0", bufs=4)
-            nc.scalar.activation(out=t["v0", n][:], in_=t["v", n][:], func=ACT.Identity,
-                                 bias=columns[:, CHUNKS + c : CHUNKS + c + 1])
-
-        def sum_squares(n):
-            t["ss", n] = psum.tile([P, 2 * TILES], F32, name="ss", tag="ss")
+        def sum_squares(n, s):
+            t["ss", n] = side_bank(s)[:, 0, 0:HEADS]
             for i in range(TILES):
                 nc.tensor.matmul(t["ss", n][:, 2 * i : 2 * i + 2], lhsT=t["sq", n][:, P * i : P * (i + 1)], rhs=head_sum[:],
                                  start=True, stop=True)
 
+        def stage_row(slot, wide, n, s):
+            nc.tensor.matmul(side_bank(s)[:, slot, :], lhsT=ident_bf[:], rhs=wide[:, chunk_cols(n)], start=True, stop=True)
+
         def rotate(n):
-            t["u", n] = psum.tile([P, TILES, P], F32, name="u", tag="u", bufs=2)
+            t["rot", n] = bank_tile([P, TILES, P], F32, "rot", "rot")
             for i in range(TILES):
-                cols = slice(P * i, P * (i + 1))
-                nc.tensor.matmul(t["u", n][:, i, :], lhsT=t["terms", n][:, 0, cols], rhs=ident[:], is_transpose=True,
+                tokens = slice(P * i, P * (i + 1))
+                nc.tensor.matmul(t["rot", n][:, i, :], lhsT=t["terms", n][:, 0, tokens], rhs=ident[:], is_transpose=True,
                                  start=True, stop=False)
-                nc.tensor.matmul(t["u", n][:, i, :], lhsT=t["terms", n][:, 1, cols], rhs=swap[:], is_transpose=True,
+                nc.tensor.matmul(t["rot", n][:, i, :], lhsT=t["terms", n][:, 1, tokens], rhs=swap[:], is_transpose=True,
                                  start=False, stop=True)
 
-        def turn_value(n):
-            t["vt", n] = psum.tile([P, TILES, P], F32, name="vt", tag="vt")
+        def transpose_value(n):
+            t["vt", n] = bank_tile([P, TILES, P], F32, "vt", "vt")
             for i in range(TILES):
                 nc.tensor.transpose(t["vt", n][:, i, :], t["v0", n][:, P * i : P * (i + 1)], ident[:])
 
-        def norm_floor(n):
-            t["ssm", n] = work.tile([P, 2 * TILES], F32, name="ssm")
-            nc.scalar.activation(out=t["ssm", n][:], in_=t["ss", n][:], func=ACT.Relu, bias=-1e-24)
+        def norm_excess(n):
+            t["excess", n] = work.tile([P, HEADS], F32, name="excess")
+            nc.scalar.activation(out=t["excess", n][:], in_=t["ss", n], func=ACT.Relu, bias=-(NORM_FLOOR**2))
 
         def norm_root(n):
-            t["nrm", n] = work.tile([P, 2 * TILES], F32, name="nrm")
-            nc.scalar.activation(out=t["nrm", n][:], in_=t["ssm", n][:], func=ACT.Sqrt, bias=1e-24)
+            t["norm", n] = work.tile([P, HEADS], F32, name="norm")
+            nc.scalar.activation(out=t["norm", n][:], in_=t["excess", n][:], func=ACT.Sqrt, bias=NORM_FLOOR**2)
 
         def norm_inverse(n):
-            t["r", n] = work.tile([P, 2 * TILES], F32, name="r")
-            nc.vector.reciprocal(out=t["r", n][:], in_=t["nrm", n][:])
-
-        def pair_tile(kind, n, bufs):
-            if n % 2 == 0:
-                t[kind, n // 2] = work.tile([P, TILES, 2 * P], F32, name=kind, bufs=bufs)
-            return t[kind, n // 2][:, :, P * (n % 2) : P * (n % 2 + 1)]
-
-        def wide_tiles(n):
-            return NV if kind(n) == "M" else NL
-
-        def pooled_tiles(n):
-            return TILES - NA if kind(n) == "M" else 0
-
-        def key_plus_bias(n):
-            c = n % CHUNKS
-            dst = pair_tile("xkb", n, 4)
-            for i in range(pooled_tiles(n), TILES):
-                for h in range(2):
-                    cols = slice(HD * h, HD * (h + 1))
-                    nc.vector.scalar_tensor_tensor(out=dst[:, i, cols], in0=t["u", n][:, i, cols],
-                                                   scalar=t["r", n][:, 2 * i + h : 2 * i + h + 1],
-                                                   in1=beta_bf[:, P * c + HD * h : P * c + HD * (h + 1)],
-                                                   op0=ALU.mult, op1=ALU.add)
+            t["inv_norm", n] = work.tile([P, HEADS], F32, name="inv_norm")
+            nc.vector.reciprocal(out=t["inv_norm", n][:], in_=t["norm", n][:])
 
         def key(n):
-            dst = pair_tile("xk", n, 4)
-            for i in range(wide_tiles(n), TILES):
-                for h in range(2):
-                    cols = slice(HD * h, HD * (h + 1))
-                    nc.scalar.activation(out=dst[:, i, cols], in_=t["u", n][:, i, cols], func=ACT.Copy,
-                                         scale=t["r", n][:, 2 * i + h : 2 * i + h + 1])
+            xk = open_pair("xk", n, 4)
+            for i, cols, q in per_head():
+                nc.scalar.activation(out=xk[:, i, cols], in_=t["rot", n][:, i, cols], func=ACT.Copy,
+                                     scale=t["inv_norm", n][:, q : q + 1])
 
-        def key_wide(n):
-            k = wide_tiles(n)
-            dst = t["xk", n // 2][:, 0:k, P * (n % 2) : P * (n % 2 + 1)]
-            for_heads = "p i (h d) -> p i h d"
-            nc.vector.tensor_tensor(out=dst.rearrange(for_heads, h=2), in0=t["u", n][:, 0:k, :].rearrange(for_heads, h=2),
-                                    in1=t["r", n][:, 0 : 2 * k].rearrange("p (i h) -> p i h", h=2).unsqueeze(3).to_broadcast([P, k, 2, HD]),
-                                    op=ALU.mult)
-
-        def add_beta(m):
-            b, cols = pair_columns(m)
-            k = pooled_tiles(2 * m)
-            nc.gpsimd.tensor_tensor(out=t["xkb", m][:, 0:k, :], in0=t["xk", m][:, 0:k, :],
-                                    in1=beta[:, cols].unsqueeze(1).to_broadcast([P, k, 2 * P]), op=ALU.add)
+        def key_plus_beta(n, s):
+            nc.vector.tensor_tensor(out=open_pair("xk_beta", n, 4), in0=half_of_pair("xk", n),
+                                    in1=side_bank(s)[:, 1:2, :].to_broadcast([P, TILES, P]), op=ALU.add)
 
         def difference(n):
             t["diff", n] = work.tile([P, TILES, P], F32, name="diff", bufs=5)
-            nc.vector.tensor_tensor(out=t["diff", n][:], in0=t["vt", n][:],
-                                    in1=t["xk", n // 2][:, :, P * (n % 2) : P * (n % 2 + 1)], op=ALU.subtract)
+            nc.vector.tensor_tensor(out=t["diff", n][:], in0=t["vt", n][:], in1=half_of_pair("xk", n), op=ALU.subtract)
 
         def statistics(n):
             t["stats", n] = work.tile([P, TILES, 6], F32, name="stats", bufs=4)
             for i in range(TILES):
                 nc.vector.bn_stats(out=t["stats", n][:, i, :], in_=t["diff", n][:, i, :].rearrange("p (h d) -> p d h", h=2))
 
-        def by_head(n):
+        def head_stats(n):
             return t["stats", n][:].rearrange("p i (h s) -> p (i h) s", h=2)
 
         def deviation(n):
-            std = work.tile([P, 2 * TILES], F32, name="std")
-            nc.scalar.activation(out=std[:], in_=by_head(n)[:, :, 2], func=ACT.Sqrt, scale=1.0 / (HD - 1))
-            t["std", n] = std
+            t["std", n] = work.tile([P, HEADS], F32, name="std")
+            nc.scalar.activation(out=t["std", n][:], in_=head_stats(n)[:, :, 2], func=ACT.Sqrt, scale=1.0 / (HD - 1))
 
-        def deviation_floor(n):
-            t["stde", n] = work.tile([P, 2 * TILES], F32, name="stde")
-            nc.scalar.activation(out=t["stde", n][:], in_=t["std", n][:], func=ACT.Copy, bias=1e-8)
+        def deviation_plus_eps(n):
+            t["std_eps", n] = work.tile([P, HEADS], F32, name="std_eps")
+            nc.scalar.activation(out=t["std_eps", n][:], in_=t["std", n][:], func=ACT.Copy, bias=STD_EPS)
 
         def deviation_inverse(n):
-            nc.vector.reciprocal(out=by_head(n)[:, :, 0], in_=t["stde", n][:])
+            nc.vector.reciprocal(out=head_stats(n)[:, :, 0], in_=t["std_eps", n][:])
 
         def shift(n):
-            t["nb", n] = work.tile([P, 2 * TILES], F32, name="nb")
-            nc.vector.tensor_reduce(out=t["nb", n][:], in_=by_head(n)[:, :, 0:2], axis=mybir.AxisListType.X, op=ALU.mult, negate=True)
+            t["shift", n] = work.tile([P, HEADS], F32, name="shift")
+            nc.vector.tensor_reduce(out=t["shift", n][:], in_=head_stats(n)[:, :, 0:2], axis=mybir.AxisListType.X,
+                                    op=ALU.mult, negate=True)
 
         def standardise(n):
-            dst = pair_tile("z", n, 3)
-            for i in range(TILES):
-                for h in range(2):
-                    cols = slice(HD * h, HD * (h + 1))
-                    q = 2 * i + h
-                    nc.scalar.activation(out=dst[:, i, cols], in_=t["diff", n][:, i, cols], func=ACT.Identity,
-                                         scale=by_head(n)[:, q, 0:1], bias=t["nb", n][:, q : q + 1])
+            z = open_pair("z", n, 3)
+            for i, cols, q in per_head():
+                nc.scalar.activation(out=z[:, i, cols], in_=t["diff", n][:, i, cols], func=ACT.Identity,
+                                     scale=head_stats(n)[:, q, 0:1], bias=t["shift", n][:, q : q + 1])
 
-        def pair_columns(m):
+        def pair_place(m):
             b, c = divmod(2 * m, CHUNKS)
             return b, slice(P * c, P * (c + 2))
 
-        def target(m):
-            b, cols = pair_columns(m)
-            zw = work.tile([P, TILES, 2 * P], F32, name="zw", bufs=2)
-            nc.gpsimd.tensor_tensor(out=zw[:], in0=t["z", m][:],
+        def store_key(m):
+            b, cols = pair_place(m)
+            nc.sync.dma_start(out=xk_hbm[b, :, :, cols], in_=t["xk", m][:])
+
+        def target_on_gpsimd(m):
+            b, cols = pair_place(m)
+            z_gamma = work.tile([P, TILES, 2 * P], F32, name="z_gamma", bufs=2)
+            nc.gpsimd.tensor_tensor(out=z_gamma[:], in0=t["z", m][:],
                                     in1=gamma[:, cols].unsqueeze(1).to_broadcast([P, TILES, 2 * P]), op=ALU.mult)
-            if pooled_tiles(2 * m + 2):
-                add_beta(m + 1)
             xv = work.tile([P, TILES, 2 * P], F32, name="xv", bufs=2)
-            nc.gpsimd.tensor_tensor(out=xv[:], in0=zw[:], in1=t["xkb", m][:], op=ALU.add)
+            nc.gpsimd.tensor_tensor(out=xv[:], in0=z_gamma[:], in1=t["xk_beta", m][:], op=ALU.add)
             nc.sync.dma_start(out=xv_hbm[b, :, :, cols], in_=xv[:])
 
-        def late_scale(n):
-            c = n % CHUNKS
-            t["zw", n] = work.tile([P, TILES, P], F32, name="zw_late", bufs=2)
-            nc.vector.tensor_tensor(out=t["zw", n][:], in0=t["z", n // 2][:, :, P * (n % 2) : P * (n % 2 + 1)],
-                                    in1=gamma[:, P * c : P * (c + 1)].unsqueeze(1).to_broadcast([P, TILES, P]), op=ALU.mult)
+        def scale_on_vector(n, s):
+            t["late_z_gamma", n] = work.tile([P, TILES, P], F32, name="late_z_gamma", bufs=2)
+            nc.vector.tensor_tensor(out=t["late_z_gamma", n][:], in0=half_of_pair("z", n),
+                                    in1=side_bank(s)[:, 2:3, :].to_broadcast([P, TILES, P]), op=ALU.mult)
 
-        def late_target(n):
-            b, c = divmod(n, CHUNKS)
-            xv = work.tile([P, TILES, P], F32, name="xv_late", bufs=4)
-            nc.vector.tensor_tensor(out=xv[:], in0=t["zw", n][:],
-                                    in1=t["xkb", n // 2][:, :, P * (n % 2) : P * (n % 2 + 1)], op=ALU.add)
-            nc.sync.dma_start(out=xv_hbm[b, :, :, P * c : P * (c + 1)], in_=xv[:])
-
-        def late(n):
-            return live(n) and kind(n) == "D"
-
-        def early(n):
-            return live(n) and kind(n) != "D"
-
-        def store_key(m):
-            b, cols = pair_columns(m)
-            nc.sync.dma_start(out=xk_hbm[b, :, :, cols], in_=t["xk", m][:])
+        def target_on_vector(n):
+            late_xv = work.tile([P, TILES, P], F32, name="late_xv", bufs=VECTOR_UNITS)
+            nc.vector.tensor_tensor(out=late_xv[:], in0=t["late_z_gamma", n][:], in1=half_of_pair("xk_beta", n), op=ALU.add)
+            nc.sync.dma_start(out=xv_hbm[n // CHUNKS, :, :, chunk_cols(n)], in_=late_xv[:])
 
         def live(n):
             return 0 <= n < UNITS
 
-        def pair_done(n):
+        def late(n):
+            return UNITS - VECTOR_UNITS <= n < UNITS
+
+        def ends_pair(n):
             return live(n) and n % 2 == 1
 
-        fed = []
-        for s in range(UNITS + LAG + 1):
-            if 1 <= s <= TILES:
-                nb, feeds = 1, [2 * s - 2, 2 * s - 1]
-            else:
-                nb, j = divmod(s + CHUNKS + 2, CHUNKS)
-                feeds = [j] if 2 <= nb < B else []
-            qb, qj = divmod(s + CHUNKS, CHUNKS)
-
+        copied = []
+        for s in range(UNITS + DEPTH):
             if live(s):
                 project("k", s)
             if live(s - 2):
-                sum_squares(s - 2)
+                sum_squares(s - 2, s)
+            if live(s - 3):
+                stage_row(1, beta_bf, s - 3, s)
+            if late(s - 6):
+                stage_row(2, gamma_bf, s - 6, s)
             if live(s - 1):
                 value(s - 1)
-            if live(s - 1):
                 rope_terms(s - 1)
             if live(s - 5):
                 deviation_inverse(s - 5)
@@ -378,22 +363,24 @@ def tile_tttwrapper_pa_kernel(tc, hidden_states, freqs_cis, wk_w_words, wk_w_sca
             if live(s):
                 project("v", s)
             if live(s - 3):
-                turn_value(s - 3)
+                transpose_value(s - 3)
             if live(s - 2):
                 rotate(s - 2)
+
+            for slot, (b, i, g) in enumerate(copied):
+                nc.scalar.copy(out=grouped_words(b, i, g), in_=xt[:, slot].rearrange("p u r -> p r u"))
+            if live(s - 2):
+                norm_excess(s - 2)
             if live(s - 1):
                 squares(s - 1)
-            if live(s - 2):
-                norm_floor(s - 2)
-            for k, (fb, j) in enumerate(fed):
-                nc.scalar.copy(out=grouped_words(fb, j % TILES, j // TILES), in_=bank[:, k].rearrange("p u r -> p r u"))
-            fed = [(nb, j) for j in feeds]
-            if feeds:
-                if feeds[0] == 0:
-                    open_batch(nb)
-                bank = psum.tile([P, len(feeds), 2, P], F32, name="xt", tag="xt")
-                for k, j in enumerate(feeds):
-                    turn(bank[:, k], nb, j % TILES, j // TILES)
+            copied = pieces_of_step(s)
+            if copied:
+                if copied[0][1:] == (0, 0):
+                    open_batch(copied[0][0])
+                xt = bank_tile([P, len(copied), 2, P], F32, "xt", "xt")
+                for slot, (b, i, g) in enumerate(copied):
+                    transpose_piece(xt[:, slot], b, i, g)
+
             if live(s - 4):
                 deviation(s - 4)
             if live(s - 2):
@@ -401,26 +388,20 @@ def tile_tttwrapper_pa_kernel(tc, hidden_states, freqs_cis, wk_w_words, wk_w_sca
             if live(s - 5):
                 standardise(s - 5)
             if live(s - 4):
-                deviation_floor(s - 4)
+                deviation_plus_eps(s - 4)
+            if late(s - 6):
+                scale_on_vector(s - 6, s)
             if live(s - 3):
-                if wide_tiles(s - 3):
-                    key_wide(s - 3)
-                key_plus_bias(s - 3)
+                key_plus_beta(s - 3, s)
+            if s % CHUNKS == QUANTISE_STEP and s // CHUNKS + 1 < B:
+                quantise(s // CHUNKS + 1)
             if live(s - 3):
                 difference(s - 3)
             if live(s - 2):
                 norm_inverse(s - 2)
-            if qb < B and qj == 6:
-                nc.vector.quantize_mx(out=codes[qb][:].rearrange("p g n -> p (g n)").bitcast(E5M2),
-                                      scales=scales[qb][:].rearrange("p g n -> p (g n)"),
-                                      in_=grouped[qb][:].rearrange("p g n -> p (g n)"))
-            if pair_done(s - 3):
+            if late(s - DEPTH):
+                target_on_vector(s - DEPTH)
+            if ends_pair(s - 3):
                 store_key((s - 3) // 2)
-            if pair_done(s - 5) and early(s - 5):
-                target((s - 5) // 2)
-            if s == 4 and pooled_tiles(0):
-                add_beta(0)
-            if late(s - LAG):
-                late_scale(s - LAG)
-            if late(s - LAG - 1):
-                late_target(s - LAG - 1)
+            if ends_pair(s - 5) and not late(s - 5):
+                target_on_gpsimd((s - 5) // 2)

from contextlib import ExitStack

import concourse.mybir as mybir
from concourse.masks import make_identity

B, L, D, HD = 4, 512, 1024, 64
FLOPS = 2 * 2 * B * L * D * D

F32 = mybir.dt.float32
BF16 = mybir.dt.bfloat16
I32 = mybir.dt.int32
U32 = mybir.dt.uint32
U8 = mybir.dt.uint8
E5M2 = mybir.dt.float8_e5m2_x4
E2M1 = mybir.dt.float4_e2m1fn_x4
ALU = mybir.AluOpType
ACT = mybir.ActivationFunctionType

P = 128
PASSES = D // 512
TILES = L // P
CHUNKS = D // P
UNITS = B * CHUNKS
HEADS = 2 * TILES
LOAD_CHUNKS = CHUNKS // 2
NORM_FLOOR = 1e-12
STD_EPS = 1e-8
VECTOR_UNITS = 4
DEPTH = 7
QUANTISE_STEP = 6


def tile_tttwrapper_pa_kernel(tc, hidden_states, freqs_cis, wk_w_words, wk_w_scales, wk_b,
                                          wv_w_words, wv_w_scales, wv_b, ttt_norm_weight, ttt_norm_bias,
                                          out_0, out_1):
    nc = tc.nc
    xk_hbm = out_0.rearrange("b (i p) h d -> b p i (h d)", p=P)
    xv_hbm = out_1.rearrange("b (i p) h d -> b p i (h d)", p=P)

    with ExitStack() as ctx:
        keep = ctx.enter_context(tc.tile_pool(name="keep", bufs=1))
        work = ctx.enter_context(tc.tile_pool(name="work", bufs=3))
        psum = ctx.enter_context(tc.psum_pool(name="psum", bufs=1))
        ctx.enter_context(tc.manual_schedule())

        banks = {"k": 2, "v": 1, "rot": 2, "vt": 1, "xt": 1, "side": 1}

        def bank_tile(shape, dtype, name, tag):
            return psum.tile(shape, dtype, name=name, tag=tag, bufs=banks[tag])

        w_scales = {}
        for kv in ("k", "v"):
            w_scales[kv] = keep.tile([P, PASSES, D], U8, name="w_scales_" + kv, align_bytes=64)
            nc.vector.memset(w_scales[kv][:].rearrange("p g n -> p (g n)").bitcast(I32), 0)
        bias_rows = keep.tile([P, P], BF16, name="bias_rows")
        nc.vector.memset(bias_rows[:], 0.0)

        ident = keep.tile([P, P], F32, name="ident")
        make_identity(nc, ident[:])
        freqs = keep.tile([P, TILES, HD], BF16, name="freqs")
        nc.scalar.dma_start(out=freqs[:], in_=freqs_cis.rearrange("(i p) j e -> p i (j e)", p=P))
        nc.gpsimd.dma_start(out=bias_rows[0:CHUNKS, :], in_=wk_b.rearrange("(c m) -> c m", m=P))
        nc.gpsimd.dma_start(out=bias_rows[CHUNKS : 2 * CHUNKS, :], in_=wv_b.rearrange("(c m) -> c m", m=P))

        x, w_words = {}, {}

        def load_x(b):
            for i in range(TILES):
                x[b, i] = keep.tile([P, D], BF16, name="x_%d_%d" % (b, i))
                nc.sync.dma_start(out=x[b, i][:], in_=hidden_states[b, P * i : P * (i + 1), :])

        def load_words(kv, src, half):
            width = 2 * P * LOAD_CHUNKS
            w_words[kv, half] = keep.tile([P, PASSES, width], U8, name="w_words_%s_%d" % (kv, half), align_bytes=64)
            nc.sync.dma_start(out=w_words[kv, half][:].bitcast(I32),
                              in_=src[:, :, width * half : width * (half + 1)].rearrange("g p n -> p g n").bitcast(I32))

        def load_scales(kv, src):
            for quad in range(4):
                nc.sync.dma_start(out=w_scales[kv][32 * quad : 32 * quad + 4, :, :].bitcast(I32),
                                  in_=src[:, 4 * quad : 4 * quad + 4, :].rearrange("g r n -> r g n").bitcast(I32))

        def load_on_all_partitions(src, name):
            wide = keep.tile([P, D], BF16, name=name)
            nc.sync.dma_start(out=wide[:], in_=src.rearrange("h d -> (h d)").partition_broadcast(P))
            return wide

        load_x(0)
        load_words("k", wk_w_words, 0)
        load_scales("k", wk_w_scales)
        load_scales("v", wv_w_scales)
        load_words("v", wv_w_words, 0)
        load_x(1)
        beta_bf = load_on_all_partitions(ttt_norm_bias, "beta_bf")
        load_words("k", wk_w_words, 1)
        load_words("v", wv_w_words, 1)
        gamma_bf = load_on_all_partitions(ttt_norm_weight, "gamma_bf")
        load_x(2)
        load_x(3)

        ident_bf = keep.tile([P, P], BF16, name="ident_bf")
        nc.vector.tensor_copy(out=ident_bf[:], in_=ident[:])
        swap = keep.tile([P, P], F32, name="swap")
        for e in range(2):
            nc.vector.tensor_copy(out=swap[:, e::2], in_=ident[:, 1 - e :: 2])
        head_sum = keep.tile([P, 2], F32, name="head_sum")
        nc.vector.memset(head_sum[:], 0.0)
        nc.vector.memset(head_sum[0:HD, 0:1], 1.0)
        nc.vector.memset(head_sum[HD:P, 1:2], 1.0)
        sign = keep.tile([P, 2], F32, name="sign")
        nc.vector.memset(sign[:, 0:1], 1.0)
        nc.vector.memset(sign[:, 1:2], -1.0)

        rope_rows = keep.tile([P, 2, TILES, P], BF16, name="rope_rows")
        cos_sin = freqs[:].rearrange("p i (j e) -> p i j e", e=2)
        pair_shape = [P, TILES, HD // 2, 2]
        for h in range(2):
            cols = slice(HD * h, HD * (h + 1))
            nc.vector.tensor_copy(out=rope_rows[:, 0, :, cols].rearrange("p i (j e) -> p i j e", e=2),
                                  in_=cos_sin[:, :, :, 0:1].to_broadcast(pair_shape))
            nc.vector.tensor_tensor(out=rope_rows[:, 1, :, cols].rearrange("p i (j e) -> p i j e", e=2),
                                    in0=cos_sin[:, :, :, 1:2].to_broadcast(pair_shape),
                                    in1=sign[:].unsqueeze(1).unsqueeze(1).to_broadcast(pair_shape), op=ALU.mult)

        grouped, x_codes, x_scales = {}, {}, {}

        def open_batch(b):
            grouped[b] = work.tile([P, PASSES, 4 * L], BF16, name="grouped", bufs=2, align_bytes=64)
            x_codes[b] = work.tile([P, PASSES, L], U32, name="x_codes", bufs=2, align_bytes=64)
            x_scales[b] = work.tile([P, PASSES, L], U8, name="x_scales", bufs=2, align_bytes=64)

        def transpose_piece(dst, b, i, g):
            x_words = x[b, i][:].bitcast(F32)
            for u in range(2):
                nc.tensor.transpose(dst[:, u, :], x_words[:, 256 * g + u : 256 * (g + 1) : 2], ident[:])

        def grouped_words(b, i, g):
            return grouped[b][:, g, 4 * P * i : 4 * P * (i + 1)].bitcast(F32).rearrange("p (r u) -> p r u", u=2)

        open_batch(0)
        first_tags = ("rot", "k", "rot", "k", "v", "xt", "rot", "k")
        for i in range(TILES):
            for g in range(PASSES):
                piece = bank_tile([P, 2, P], F32, "first_piece", first_tags[PASSES * i + g])
                transpose_piece(piece, 0, i, g)
                if g == 0:
                    nc.scalar.copy(out=grouped_words(0, i, g), in_=piece[:].rearrange("p u r -> p r u"))
                else:
                    nc.vector.tensor_copy(out=grouped_words(0, i, g), in_=piece[:].rearrange("p u r -> p r u"))
        rope_t = bank_tile([P, 2, L], BF16, "rope_t", "vt")
        for cs in range(2):
            for i in range(TILES):
                nc.tensor.transpose(rope_t[:, cs, P * i : P * (i + 1)], rope_rows[:, cs, i, :], ident_bf[:])
        bias_t = bank_tile([P, P], BF16, "bias_t", "side")
        nc.tensor.transpose(bias_t[:], bias_rows[:], ident_bf[:])
        rope = keep.tile([P, 2, L], BF16, name="rope")
        nc.scalar.copy(out=rope[:], in_=rope_t[:])
        bias = keep.tile([P, 2 * CHUNKS], F32, name="bias")
        nc.scalar.copy(out=bias[:], in_=bias_t[:, 0 : 2 * CHUNKS])
        for g in range(PASSES):
            nc.vector.quantize_mx(out=x_codes[0][:, g, :].bitcast(E5M2), scales=x_scales[0][:, g, :], in_=grouped[0][:, g, :])
        gamma = keep.tile([P, D], F32, name="gamma")
        nc.gpsimd.tensor_scalar(out=gamma[:], in0=gamma_bf[:], scalar1=1.0, scalar2=0.0, op0=ALU.mult, op1=ALU.add)

        def quantise(b):
            nc.vector.quantize_mx(out=x_codes[b][:].rearrange("p g n -> p (g n)").bitcast(E5M2),
                                  scales=x_scales[b][:].rearrange("p g n -> p (g n)"),
                                  in_=grouped[b][:].rearrange("p g n -> p (g n)"))

        def pieces_of_step(s):
            if 1 <= s <= TILES:
                b, numbers = 1, [2 * s - 2, 2 * s - 1]
            else:
                b, j = divmod(s + CHUNKS + 2, CHUNKS)
                numbers = [j] if 2 <= b < B else []
            return [(b, j % TILES, j // TILES) for j in numbers]

        t = {}

        def chunk_cols(n):
            c = n % CHUNKS
            return slice(P * c, P * (c + 1))

        def per_head():
            return [(i, slice(HD * h, HD * (h + 1)), 2 * i + h) for i in range(TILES) for h in range(2)]

        def half_of_pair(kind, n):
            return t[kind, n // 2][:, :, P * (n % 2) : P * (n % 2 + 1)]

        def open_pair(kind, n, bufs):
            if n % 2 == 0:
                t[kind, n // 2] = work.tile([P, TILES, 2 * P], F32, name=kind, bufs=bufs)
            return half_of_pair(kind, n)

        def side_bank(s):
            if ("side", s) not in t:
                t["side", s] = bank_tile([P, 3, P], F32, "side", "side")
            return t["side", s]

        def project(kv, n):
            b, c = divmod(n, CHUNKS)
            half, c_in = divmod(c, LOAD_CHUNKS)
            t[kv, n] = bank_tile([P, L], F32, "proj_" + kv, kv)
            for g in range(PASSES):
                nc.tensor.matmul_mx(out=t[kv, n][:],
                                    lhsT=w_words[kv, half][:, g, 2 * P * c_in : 2 * P * (c_in + 1)].bitcast(E2M1),
                                    lhsT_scale=w_scales[kv][:, g, chunk_cols(n)],
                                    rhs=x_codes[b][:, g, :].bitcast(E5M2), rhs_scale=x_scales[b][:, g, :],
                                    start=(g == 0), stop=(g == PASSES - 1))

        def value(n):
            c = CHUNKS + n % CHUNKS
            t["v0", n] = work.tile([P, L], F32, name="v0", bufs=4)
            nc.scalar.activation(out=t["v0", n][:], in_=t["v", n][:], func=ACT.Identity, bias=bias[:, c : c + 1])

        def rope_terms(n):
            c = n % CHUNKS
            t["terms", n] = work.tile([P, 2, L], F32, name="terms")
            nc.vector.scalar_tensor_tensor(out=t["terms", n][:], in0=t["k", n][:].unsqueeze(1).to_broadcast([P, 2, L]),
                                           scalar=bias[:, c : c + 1], in1=rope[:], op0=ALU.add, op1=ALU.mult)

        def squares(n):
            c = n % CHUNKS
            t["sq", n] = work.tile([P, L], F32, name="sq")
            nc.scalar.activation(out=t["sq", n][:], in_=t["k", n][:], func=ACT.Square, bias=bias[:, c : c + 1])

        def sum_squares(n, s):
            t["ss", n] = side_bank(s)[:, 0, 0:HEADS]
            for i in range(TILES):
                nc.tensor.matmul(t["ss", n][:, 2 * i : 2 * i + 2], lhsT=t["sq", n][:, P * i : P * (i + 1)], rhs=head_sum[:],
                                 start=True, stop=True)

        def stage_row(slot, wide, n, s):
            nc.tensor.matmul(side_bank(s)[:, slot, :], lhsT=ident_bf[:], rhs=wide[:, chunk_cols(n)], start=True, stop=True)

        def rotate(n):
            t["rot", n] = bank_tile([P, TILES, P], F32, "rot", "rot")
            for i in range(TILES):
                tokens = slice(P * i, P * (i + 1))
                nc.tensor.matmul(t["rot", n][:, i, :], lhsT=t["terms", n][:, 0, tokens], rhs=ident[:], is_transpose=True,
                                 start=True, stop=False)
                nc.tensor.matmul(t["rot", n][:, i, :], lhsT=t["terms", n][:, 1, tokens], rhs=swap[:], is_transpose=True,
                                 start=False, stop=True)

        def transpose_value(n):
            t["vt", n] = bank_tile([P, TILES, P], F32, "vt", "vt")
            for i in range(TILES):
                nc.tensor.transpose(t["vt", n][:, i, :], t["v0", n][:, P * i : P * (i + 1)], ident[:])

        def norm_excess(n):
            t["excess", n] = work.tile([P, HEADS], F32, name="excess")
            nc.scalar.activation(out=t["excess", n][:], in_=t["ss", n], func=ACT.Relu, bias=-(NORM_FLOOR**2))

        def norm_root(n):
            t["norm", n] = work.tile([P, HEADS], F32, name="norm")
            nc.scalar.activation(out=t["norm", n][:], in_=t["excess", n][:], func=ACT.Sqrt, bias=NORM_FLOOR**2)

        def norm_inverse(n):
            t["inv_norm", n] = work.tile([P, HEADS], F32, name="inv_norm")
            nc.vector.reciprocal(out=t["inv_norm", n][:], in_=t["norm", n][:])

        def key(n):
            xk = open_pair("xk", n, 4)
            for i, cols, q in per_head():
                nc.scalar.activation(out=xk[:, i, cols], in_=t["rot", n][:, i, cols], func=ACT.Copy,
                                     scale=t["inv_norm", n][:, q : q + 1])

        def key_plus_beta(n, s):
            nc.vector.tensor_tensor(out=open_pair("xk_beta", n, 4), in0=half_of_pair("xk", n),
                                    in1=side_bank(s)[:, 1:2, :].to_broadcast([P, TILES, P]), op=ALU.add)

        def difference(n):
            t["diff", n] = work.tile([P, TILES, P], F32, name="diff", bufs=5)
            nc.vector.tensor_tensor(out=t["diff", n][:], in0=t["vt", n][:], in1=half_of_pair("xk", n), op=ALU.subtract)

        def statistics(n):
            t["stats", n] = work.tile([P, TILES, 6], F32, name="stats", bufs=4)
            for i in range(TILES):
                nc.vector.bn_stats(out=t["stats", n][:, i, :], in_=t["diff", n][:, i, :].rearrange("p (h d) -> p d h", h=2))

        def head_stats(n):
            return t["stats", n][:].rearrange("p i (h s) -> p (i h) s", h=2)

        def deviation(n):
            t["std", n] = work.tile([P, HEADS], F32, name="std")
            nc.scalar.activation(out=t["std", n][:], in_=head_stats(n)[:, :, 2], func=ACT.Sqrt, scale=1.0 / (HD - 1))

        def deviation_plus_eps(n):
            t["std_eps", n] = work.tile([P, HEADS], F32, name="std_eps")
            nc.scalar.activation(out=t["std_eps", n][:], in_=t["std", n][:], func=ACT.Copy, bias=STD_EPS)

        def deviation_inverse(n):
            nc.vector.reciprocal(out=head_stats(n)[:, :, 0], in_=t["std_eps", n][:])

        def shift(n):
            t["shift", n] = work.tile([P, HEADS], F32, name="shift")
            nc.vector.tensor_reduce(out=t["shift", n][:], in_=head_stats(n)[:, :, 0:2], axis=mybir.AxisListType.X,
                                    op=ALU.mult, negate=True)

        def standardise(n):
            z = open_pair("z", n, 3)
            for i, cols, q in per_head():
                nc.scalar.activation(out=z[:, i, cols], in_=t["diff", n][:, i, cols], func=ACT.Identity,
                                     scale=head_stats(n)[:, q, 0:1], bias=t["shift", n][:, q : q + 1])

        def pair_place(m):
            b, c = divmod(2 * m, CHUNKS)
            return b, slice(P * c, P * (c + 2))

        def store_key(m):
            b, cols = pair_place(m)
            nc.sync.dma_start(out=xk_hbm[b, :, :, cols], in_=t["xk", m][:])

        def target_on_gpsimd(m):
            b, cols = pair_place(m)
            z_gamma = work.tile([P, TILES, 2 * P], F32, name="z_gamma", bufs=2)
            nc.gpsimd.tensor_tensor(out=z_gamma[:], in0=t["z", m][:],
                                    in1=gamma[:, cols].unsqueeze(1).to_broadcast([P, TILES, 2 * P]), op=ALU.mult)
            xv = work.tile([P, TILES, 2 * P], F32, name="xv", bufs=2)
            nc.gpsimd.tensor_tensor(out=xv[:], in0=z_gamma[:], in1=t["xk_beta", m][:], op=ALU.add)
            nc.sync.dma_start(out=xv_hbm[b, :, :, cols], in_=xv[:])

        def scale_on_vector(n, s):
            t["late_z_gamma", n] = work.tile([P, TILES, P], F32, name="late_z_gamma", bufs=2)
            nc.vector.tensor_tensor(out=t["late_z_gamma", n][:], in0=half_of_pair("z", n),
                                    in1=side_bank(s)[:, 2:3, :].to_broadcast([P, TILES, P]), op=ALU.mult)

        def target_on_vector(n):
            late_xv = work.tile([P, TILES, P], F32, name="late_xv", bufs=VECTOR_UNITS)
            nc.vector.tensor_tensor(out=late_xv[:], in0=t["late_z_gamma", n][:], in1=half_of_pair("xk_beta", n), op=ALU.add)
            nc.sync.dma_start(out=xv_hbm[n // CHUNKS, :, :, chunk_cols(n)], in_=late_xv[:])

        def live(n):
            return 0 <= n < UNITS

        def late(n):
            return UNITS - VECTOR_UNITS <= n < UNITS

        def ends_pair(n):
            return live(n) and n % 2 == 1

        copied = []
        for s in range(UNITS + DEPTH):
            if live(s):
                project("k", s)
            if live(s - 2):
                sum_squares(s - 2, s)
            if live(s - 3):
                stage_row(1, beta_bf, s - 3, s)
            if late(s - 6):
                stage_row(2, gamma_bf, s - 6, s)
            if live(s - 1):
                value(s - 1)
                rope_terms(s - 1)
            if live(s - 5):
                deviation_inverse(s - 5)
            if live(s - 3):
                key(s - 3)
            if live(s - 4):
                statistics(s - 4)
            if live(s - 5):
                shift(s - 5)
            if live(s):
                project("v", s)
            if live(s - 3):
                transpose_value(s - 3)
            if live(s - 2):
                rotate(s - 2)

            for slot, (b, i, g) in enumerate(copied):
                nc.scalar.copy(out=grouped_words(b, i, g), in_=xt[:, slot].rearrange("p u r -> p r u"))
            if live(s - 2):
                norm_excess(s - 2)
            if live(s - 1):
                squares(s - 1)
            copied = pieces_of_step(s)
            if copied:
                if copied[0][1:] == (0, 0):
                    open_batch(copied[0][0])
                xt = bank_tile([P, len(copied), 2, P], F32, "xt", "xt")
                for slot, (b, i, g) in enumerate(copied):
                    transpose_piece(xt[:, slot], b, i, g)

            if live(s - 4):
                deviation(s - 4)
            if live(s - 2):
                norm_root(s - 2)
            if live(s - 5):
                standardise(s - 5)
            if live(s - 4):
                deviation_plus_eps(s - 4)
            if late(s - 6):
                scale_on_vector(s - 6, s)
            if live(s - 3):
                key_plus_beta(s - 3, s)
            if s % CHUNKS == QUANTISE_STEP and s // CHUNKS + 1 < B:
                quantise(s // CHUNKS + 1)
            if live(s - 3):
                difference(s - 3)
            if live(s - 2):
                norm_inverse(s - 2)
            if late(s - DEPTH):
                target_on_vector(s - DEPTH)
            if ends_pair(s - 3):
                store_key((s - 3) // 2)
            if ends_pair(s - 5) and not late(s - 5):
                target_on_gpsimd((s - 5) // 2)
